import numpy as np
import ml_dtypes


def mxq(x, axis, fmt="e4m3"):
    dtype, down = {"e4m3": (ml_dtypes.float8_e4m3fn, 7), "e5m2": (ml_dtypes.float8_e5m2, 14)}[fmt]
    v = np.moveaxis(np.asarray(x, np.float32).astype(ml_dtypes.bfloat16).astype(np.float64), axis, -1)
    blocks = v.reshape(v.shape[:-1] + (-1, 32))
    amax = np.abs(blocks).max(-1, keepdims=True)
    byte = np.maximum(np.where(amax > 0, np.frexp(amax)[1] - 1 + 127, 0) - down, 1)
    scale = np.exp2(byte - 127.0)
    codes = (blocks / scale).astype(np.float32).astype(dtype).astype(np.float64)
    return np.moveaxis((codes * scale).reshape(v.shape), -1, axis)


WIDE = False


def mx_kscale(k):
    if not WIDE:
        return np.ones(k)
    levels = np.array([18, -18])
    if k % 512:
        return np.exp2(np.random.permutation(np.resize(levels, k // 32))).repeat(32)
    a = np.empty((k // 512, 16))
    for p in range(k // 512):
        a[p, :8] = np.random.permutation(np.resize(levels, 8))
        for g in range(8):
            far = levels[np.abs(levels - a[p, g]) >= 10]
            a[p, g + 8] = far[np.random.randint(len(far))]
    return np.exp2(a.ravel()).repeat(32)


BF16 = ml_dtypes.bfloat16


def bf(x):
    return np.asarray(x, np.float32).astype(BF16)


def f64(x):
    return np.asarray(x).astype(np.float64)


B, S, D_IN, D_OUT, R = 4, 256, 1024, 1024, 128
T = B * S
SCALING = 2.0


def setup_inputs():
    s = mx_kscale(T)
    s = (s / s.min()).reshape(B, S, 1)
    u = mx_kscale(D_OUT)
    x0 = bf(np.random.standard_normal((B, S, D_IN)))
    w0 = bf(np.random.standard_normal((D_OUT, D_IN)) / np.sqrt(D_IN))
    a_w = bf(np.random.standard_normal((R, D_IN)) / np.sqrt(D_IN))
    b_w = bf(np.random.standard_normal((D_OUT, R)) / np.sqrt(R))
    magnitude = bf(np.random.uniform(size=(1, D_OUT)) + 0.5)
    h_lora = bf(np.random.standard_normal((B, S, R)))
    g = bf(4.0 * np.random.standard_normal((B, S, D_OUT)) * np.exp2(np.random.randint(-6, 1, (B, S, 1))) / s * u)
    pre = f64(x0) @ f64(w0).T + SCALING * (f64(h_lora) @ f64(b_w).T)
    w_eff = f64(w0) + SCALING * (f64(b_w) @ f64(a_w))
    weight_norm = np.sqrt((w_eff * w_eff).sum(axis=1))
    return {"x": bf(f64(x0) * s), "weight": bf(f64(w0) / u[:, None]), "a_w": a_w, "b_w": b_w,
            "magnitude": magnitude, "h_lora": h_lora,
            "pre": np.asarray(pre, np.float32), "w_eff": np.asarray(w_eff, np.float32),
            "weight_norm": np.asarray(weight_norm, np.float32), "grad_out": g}


def reference(x, weight, a_w, b_w, magnitude, h_lora, pre, w_eff, weight_norm, grad_out):
    xf = f64(x).reshape(T, D_IN)
    g = f64(grad_out).reshape(T, D_OUT)
    p = f64(pre).reshape(T, D_OUT)
    n = f64(weight_norm)
    m = f64(magnitude).reshape(-1) / n
    dz = g * m
    dx = mxq(dz, 1, "e5m2") @ mxq(f64(weight), 0, "e4m3")
    dw = mxq(dz, 0, "e5m2").T @ mxq(xf, 0, "e4m3")
    c = (g * p).sum(axis=0) * m / (n * n)
    dw = dw - c[:, None] * f64(w_eff)
    return dx.reshape(B, S, D_IN), dw

@@ -1,0 +1,228 @@
+from contextlib import ExitStack
+
+import concourse.mybir as mybir
+from concourse.masks import make_identity
+
+T, D_IN, D_OUT = 1024, 1024, 1024
+FLOPS = 2 * 2 * T * D_IN * D_OUT
+BYTES = 2 * (T * D_IN + D_OUT * D_IN + T * D_OUT + D_OUT) + 4 * (T * D_OUT + D_OUT * D_IN + D_OUT) + 4 * (T * D_IN + D_OUT * D_IN)
+
+F32 = mybir.dt.float32
+BF16 = mybir.dt.bfloat16
+U32 = mybir.dt.uint32
+U8 = mybir.dt.uint8
+E4M3X4 = mybir.dt.float8_e4m3fn_x4
+E5M2X4 = mybir.dt.float8_e5m2_x4
+MULT = mybir.AluOpType.mult
+ADD = mybir.AluOpType.add
+COPY = mybir.ActivationFunctionType.Copy
+
+P = 128
+J = 4
+K = P * J
+H = 512
+
+
+def tile_loralinear_pa_v_kernel(tc, x, weight, a_w, b_w, magnitude, h_lora, pre, w_eff, weight_norm, grad_out, out_0, out_1):
+    nc = tc.nc
+    x_v = x.flatten_outer_dims().rearrange("(g p j) d -> g p j d", p=P, j=J)
+    g_v = grad_out.flatten_outer_dims().rearrange("(g p j) d -> g p j d", p=P, j=J)
+    p_v = pre.flatten_outer_dims().rearrange("(g p j) d -> g p j d", p=P, j=J)
+    w_v = weight.rearrange("(g p j) d -> g p j d", p=P, j=J)
+    we_v = w_eff.rearrange("(b q) d -> b q d", q=P)
+    o0_v = out_0.flatten_outer_dims().rearrange("(g p j) d -> g j p d", p=P, j=J)
+    o1_v = out_1.rearrange("(b q) d -> b q d", q=P)
+
+    with ExitStack() as ctx:
+        sb = ctx.enter_context(tc.tile_pool(name="sb", bufs=1))
+        ps = ctx.enter_context(tc.psum_pool(name="ps", bufs=1))
+
+        ident = sb.tile([P, P], F32, name="ident")
+        make_identity(nc, ident[:])
+        norm8 = sb.tile([8, P], F32, name="norm8")
+        mag8 = sb.tile([8, P], BF16, name="mag8")
+        rows = sb.tile([P, 2, P], F32, name="rows")
+        rcol = sb.tile([P, 8], F32, name="rcol")
+        mcol = sb.tile([P, 8], F32, name="mcol")
+        r2col = sb.tile([P, 8], F32, name="r2col")
+        kcol = sb.tile([P, 8], F32, name="kcol")
+        kneg = sb.tile([P, 8], F32, name="kneg")
+        cpart = sb.tile([P, 16], F32, name="cpart")
+        csum = sb.tile([P, 8], F32, name="csum")
+        negc = sb.tile([P, 8], F32, name="negc")
+
+        t_codes = [sb.tile([P, D_OUT], U32, name="t_codes%d" % g, align_bytes=64) for g in range(2)]
+        t_scale = [sb.tile([P, D_OUT], U8, name="t_scale%d" % g, align_bytes=64) for g in range(2)]
+        f_codes = [sb.tile([P, T], U32, name="f_codes%d" % g, align_bytes=64) for g in range(2)]
+        f_scale = [sb.tile([P, T], U8, name="f_scale%d" % g, align_bytes=64) for g in range(2)]
+        w_codes = [sb.tile([P, D_IN], U32, name="w_codes%d" % g, align_bytes=64) for g in range(2)]
+        w_scale = [sb.tile([P, D_IN], U8, name="w_scale%d" % g, align_bytes=64) for g in range(2)]
+        x_codes = [sb.tile([P, D_IN], U32, name="x_codes%d" % g, align_bytes=64) for g in range(2)]
+        x_scale = [sb.tile([P, D_IN], U8, name="x_scale%d" % g, align_bytes=64) for g in range(2)]
+
+        g_raw, w_raw, x_raw, p_raw, we_raw = {}, {}, {}, {}, {}
+        t_il, w_il, x_il, f_il, gp, m_bank = {}, {}, {}, {}, {}, {}
+
+        def load(store, key, view, dtype, tag, bufs):
+            t = sb.tile([P, J, 1024], dtype, name="%s%d" % (tag, key), tag=tag, bufs=bufs)
+            nc.sync.dma_start(out=t[:], in_=view)
+            store[key] = t
+
+        def il_tile(store, g, name, tag):
+            store[g] = sb.tile([P, 1024, J], BF16, name="%s%d" % (name, g), tag=tag, bufs=2, align_bytes=64)
+
+        def interleave(engine, store, raw, g, h):
+            cols = slice(h * H, (h + 1) * H)
+            out = store[g][:, cols, :].rearrange("p (c i) j -> p c j i", i=4)
+            in_ = raw[g][:, :, cols].rearrange("p j (c i) -> p c j i", i=4)
+            if engine == "v":
+                nc.vector.tensor_copy(out=out, in_=in_)
+            elif engine == "s":
+                nc.scalar.copy(out=out, in_=in_)
+            else:
+                nc.gpsimd.tensor_scalar(out=store[g][:, cols, :], in0=raw[g][:, :, cols].rearrange("p j d -> p d j"), scalar1=1.0, scalar2=1.0, op0=MULT, op1=MULT)
+
+        def quantize(codes, scales, t, fmt):
+            nc.vector.quantize_mx(out=codes[:].bitcast(fmt), scales=scales[:], in_=t[:].rearrange("p w j -> p (w j)"))
+
+        def make_dz(g, h):
+            cols = slice(h * H, (h + 1) * H)
+            nc.vector.tensor_tensor(out=t_il[g][:, cols, :].rearrange("p (c i) j -> p c j i", i=4),
+                                    in0=g_raw[g][:, :, cols].rearrange("p j (c i) -> p c j i", i=4),
+                                    in1=m_bank[h][:].rearrange("p (c i) -> p c i", i=4).unsqueeze(2).to_broadcast([P, H // 4, J, 4]), op=MULT)
+
+        def transpose_dz(g, h):
+            words = t_il[g][:, h * H:(h + 1) * H, :].rearrange("p o j -> p (o j)").bitcast(F32)
+            f_v = f_il[g][:, h * H:(h + 1) * H, :].rearrange("q (u e p) t -> q u e p t", u=2, e=2)
+            for u in range(2):
+                xt = ps.tile([P, J, P], F32, name="xt", tag="xt", bufs=2)
+                for i in range(4):
+                    w0 = 2 * i + u
+                    nc.tensor.transpose(xt[:, i, :], words[:, w0:w0 + 8 * 127 + 1:8], ident[:])
+                nc.scalar.copy(out=f_v[:, u], in_=xt[:].rearrange("q t p -> q (t p)").bitcast(BF16).rearrange("q (t p e) -> q e p t", t=4, e=2))
+
+        def matmul_0(g):
+            for j in range(J):
+                r = sb.tile([P, D_IN], F32, name="r0", tag="r0", bufs=4)
+                for n in range(2):
+                    n_cols = slice(n * H, (n + 1) * H)
+                    acc = ps.tile([P, H], F32, name="acc", tag="acc", bufs=4)
+                    for q in range(2):
+                        m_cols = slice(q * H + j * P, q * H + (j + 1) * P)
+                        nc.tensor.matmul_mx(out=acc[:], lhsT=f_codes[g][:, m_cols].bitcast(E5M2X4), lhsT_scale=f_scale[g][:, m_cols],
+                                            rhs=w_codes[q][:, n_cols].bitcast(E4M3X4), rhs_scale=w_scale[q][:, n_cols],
+                                            start=(q == 0), stop=(q == 1))
+                    nc.scalar.copy(out=r[:, n_cols], in_=acc[:])
+                nc.sync.dma_start(out=o0_v[g, j], in_=r[:])
+
+        def make_gp(g, h):
+            cols = slice(h * H, (h + 1) * H)
+            t = sb.tile([P, J, H], F32, name="gp%d%d" % (g, h), tag="gp", bufs=3)
+            nc.vector.tensor_tensor(out=t[:], in0=g_raw[g][:, :, cols], in1=p_raw[g][:, :, cols], op=MULT)
+            gp[g, h] = t
+
+        def sum_gp(g, h):
+            for b in range(4):
+                gt = ps.tile([P, J, P], F32, name="gt", tag=("m", "xt")[b % 2], bufs=2)
+                for j in range(J):
+                    nc.tensor.transpose(gt[:, j, :], gp[g, h][:, j, b * P:(b + 1) * P], ident[:])
+                junk = sb.tile([P, H], BF16, name="junk", tag="junk", bufs=2)
+                i = g * 8 + h * 4 + b
+                nc.scalar.activation(out=junk[:], in_=gt[:].rearrange("q j p -> q (j p)"), func=COPY, accum_out=cpart[:, i:i + 1])
+
+        def matmul_1(b):
+            h, b4 = divmod(b, 4)
+            m_cols = slice(b * P, (b + 1) * P)
+            for n in range(2):
+                n_cols = slice(n * H, (n + 1) * H)
+                acc = ps.tile([P, H], F32, name="acc", tag="acc", bufs=4)
+                for g in range(2):
+                    nc.tensor.matmul_mx(out=acc[:], lhsT=t_codes[g][:, m_cols].bitcast(E5M2X4), lhsT_scale=t_scale[g][:, m_cols],
+                                        rhs=x_codes[g][:, n_cols].bitcast(E4M3X4), rhs_scale=x_scale[g][:, n_cols],
+                                        start=(g == 0), stop=(g == 1))
+                w = we_raw[b][:, n_cols]
+                nc.vector.scalar_tensor_tensor(out=w, in0=w, scalar=negc[:, b:b + 1], in1=acc[:], op0=MULT, op1=ADD)
+                if b == 7:
+                    nc.sync.dma_start(out=o1_v[b][:, n_cols], in_=w)
+            if b < 7:
+                nc.sync.dma_start(out=o1_v[b], in_=we_raw[b])
+
+        def correction(h):
+            cols = slice(4 * h, 4 * h + 4)
+            nc.gpsimd.tensor_tensor(out=csum[:, cols], in0=cpart[:, cols], in1=cpart[:, 8 + 4 * h:12 + 4 * h], op=ADD)
+            nc.gpsimd.tensor_tensor(out=negc[:, cols], in0=csum[:, cols], in1=kneg[:, cols], op=MULT)
+
+        with tc.manual_schedule():
+            nc.sync.dma_start(out=norm8[:], in_=weight_norm.rearrange("(b q) -> b q", q=P))
+            nc.scalar.dma_start(out=mag8[:], in_=magnitude.rearrange("a (b q) -> (a b) q", q=P))
+            nc.vector.memset(rows[:], 0.0)
+            load(g_raw, 0, g_v[0], BF16, "g_raw", 2)
+            load(w_raw, 0, w_v[0], BF16, "raw", 3)
+            load(g_raw, 1, g_v[1], BF16, "g_raw", 2)
+            load(w_raw, 1, w_v[1], BF16, "raw", 3)
+            load(p_raw, 0, p_v[0], F32, "big", 3)
+            load(p_raw, 1, p_v[1], F32, "big", 3)
+            load(x_raw, 2, x_v[0], BF16, "raw", 3)
+            load(x_raw, 3, x_v[1], BF16, "raw", 3)
+            x_raw[0], x_raw[1] = x_raw[2], x_raw[3]
+            for h in range(2):
+                t = sb.tile([P, 4, D_IN], F32, name="we%d" % h, tag="big", bufs=3)
+                for b4 in range(4):
+                    b = 4 * h + b4
+                    nc.sync.dma_start(out=t[:, b4, :], in_=we_v[b])
+                    we_raw[b] = t[:, b4, :]
+
+            nc.vector.tensor_copy(out=rows[0:8, 0, :], in_=norm8[:])
+            nc.vector.tensor_copy(out=rows[0:8, 1, :], in_=mag8[:])
+            nt = ps.tile([P, 2, P], F32, name="nt", tag="xt", bufs=2)
+            nc.tensor.transpose(nt[:, 0, :], rows[:, 0, :], ident[:])
+            nc.tensor.transpose(nt[:, 1, :], rows[:, 1, :], ident[:])
+            nc.vector.reciprocal(out=rcol[:], in_=nt[:, 0, 0:8])
+            nc.vector.tensor_tensor(out=mcol[:], in0=nt[:, 1, 0:8], in1=rcol[:], op=MULT)
+            for h in range(2):
+                bank = ps.tile([P, H], F32, name="mb%d" % h, tag="m", bufs=2)
+                for b in range(4):
+                    i = h * 4 + b
+                    nc.tensor.transpose(bank[:, b * P:(b + 1) * P], mcol[:, i:i + 1].to_broadcast([P, P]), ident[:])
+                m_bank[h] = bank
+
+            for g in range(2):
+                il_tile(w_il, g, "w_il", "il")
+            interleave("s", w_il, w_raw, 0, 0)
+            interleave("g", w_il, w_raw, 0, 1)
+            interleave("g", w_il, w_raw, 1, 0)
+            interleave("g", w_il, w_raw, 1, 1)
+            for g in range(2):
+                il_tile(t_il, g, "t_il", "t_il")
+                il_tile(f_il, g, "f_il", "f_il")
+                for h in range(2):
+                    make_dz(g, h)
+                    transpose_dz(g, h)
+            nc.gpsimd.tensor_tensor(out=r2col[:], in0=rcol[:], in1=rcol[:], op=MULT)
+            nc.gpsimd.tensor_tensor(out=kcol[:], in0=r2col[:], in1=mcol[:], op=MULT)
+            nc.gpsimd.tensor_scalar(out=kneg[:], in0=kcol[:], scalar1=-1.0, scalar2=1.0, op0=MULT, op1=MULT)
+            for g, h in ((0, 0), (0, 1), (1, 0)):
+                make_gp(g, h)
+                sum_gp(g, h)
+            quantize(w_codes[0], w_scale[0], w_il[0], E4M3X4)
+            quantize(f_codes[0], f_scale[0], f_il[0], E5M2X4)
+            quantize(w_codes[1], w_scale[1], w_il[1], E4M3X4)
+            make_gp(1, 1)
+            matmul_0(0)
+            sum_gp(1, 1)
+            for g in range(2):
+                il_tile(x_il, g, "x_il", "il")
+            interleave("v", x_il, x_raw, 0, 0)
+            quantize(f_codes[1], f_scale[1], f_il[1], E5M2X4)
+            interleave("v", x_il, x_raw, 0, 1)
+            quantize(t_codes[0], t_scale[0], t_il[0], E5M2X4)
+            interleave("v", x_il, x_raw, 1, 0)
+            quantize(x_codes[0], x_scale[0], x_il[0], E4M3X4)
+            interleave("v", x_il, x_raw, 1, 1)
+            quantize(t_codes[1], t_scale[1], t_il[1], E5M2X4)
+            correction(0)
+            quantize(x_codes[1], x_scale[1], x_il[1], E4M3X4)
+            correction(1)
+            matmul_0(1)
+            for b in range(8):
+                matmul_1(b)

@@ -29,9 +29,9 @@ def tile_loralinear_pa_v_kernel(tc, x, weight, a_w, b_w, magnitude, h_lora, pre,
     g_v = grad_out.flatten_outer_dims().rearrange("(g p j) d -> g p j d", p=P, j=J)
     p_v = pre.flatten_outer_dims().rearrange("(g p j) d -> g p j d", p=P, j=J)
     w_v = weight.rearrange("(g p j) d -> g p j d", p=P, j=J)
-    we_v = w_eff.rearrange("(b q) d -> b q d", q=P)
-    o0_v = out_0.flatten_outer_dims().rearrange("(g p j) d -> g j p d", p=P, j=J)
-    o1_v = out_1.rearrange("(b q) d -> b q d", q=P)
+    we_v = w_eff.rearrange("(h b q) d -> h q b d", q=P, b=4)
+    o0_v = out_0.flatten_outer_dims().rearrange("(g p j) d -> g p j d", p=P, j=J)
+    o1_v = out_1.rearrange("(h b q) d -> h q b d", q=P, b=4)
 
     with ExitStack() as ctx:
         sb = ctx.enter_context(tc.tile_pool(name="sb", bufs=1))
@@ -47,9 +47,8 @@ def tile_loralinear_pa_v_kernel(tc, x, weight, a_w, b_w, magnitude, h_lora, pre,
         r2col = sb.tile([P, 8], F32, name="r2col")
         kcol = sb.tile([P, 8], F32, name="kcol")
         kneg = sb.tile([P, 8], F32, name="kneg")
-        cpart = sb.tile([P, 16], F32, name="cpart")
-        csum = sb.tile([P, 8], F32, name="csum")
         negc = sb.tile([P, 8], F32, name="negc")
+        junk = sb.tile([P, 8, P], BF16, name="junk")
 
         t_codes = [sb.tile([P, D_OUT], U32, name="t_codes%d" % g, align_bytes=64) for g in range(2)]
         t_scale = [sb.tile([P, D_OUT], U8, name="t_scale%d" % g, align_bytes=64) for g in range(2)]
@@ -61,10 +60,18 @@ def tile_loralinear_pa_v_kernel(tc, x, weight, a_w, b_w, magnitude, h_lora, pre,
         x_scale = [sb.tile([P, D_IN], U8, name="x_scale%d" % g, align_bytes=64) for g in range(2)]
 
         g_raw, w_raw, x_raw, p_raw, we_raw = {}, {}, {}, {}, {}
-        t_il, w_il, x_il, f_il, gp, m_bank = {}, {}, {}, {}, {}, {}
+        t_il, w_il, x_il, f_il, m_bank, c_bank, r0 = {}, {}, {}, {}, {}, {}, {}
 
-        def load(store, key, view, dtype, tag, bufs):
-            t = sb.tile([P, J, 1024], dtype, name="%s%d" % (tag, key), tag=tag, bufs=bufs)
+        turn = {"xt": 0, "acc0": 0, "acc1": 0}
+        banks = {"xt": (2, 3, 4, 5), "acc0": (6, 7, 2, 3, 4, 5), "acc1": (2, 3, 4, 5, 6, 7, 0, 1)}
+
+        def bank_tile(role, shape):
+            i = banks[role][turn[role] % len(banks[role])]
+            turn[role] = turn[role] + 1
+            return ps.tile(shape, F32, name=role, tag="bank%d" % i, bufs=1)
+
+        def load(store, key, view, dtype, name):
+            t = sb.tile([P, J, 1024], dtype, name="%s%d" % (name, key))
             nc.sync.dma_start(out=t[:], in_=view)
             store[key] = t
 
@@ -95,134 +102,128 @@ def tile_loralinear_pa_v_kernel(tc, x, weight, a_w, b_w, magnitude, h_lora, pre,
             words = t_il[g][:, h * H:(h + 1) * H, :].rearrange("p o j -> p (o j)").bitcast(F32)
             f_v = f_il[g][:, h * H:(h + 1) * H, :].rearrange("q (u e p) t -> q u e p t", u=2, e=2)
             for u in range(2):
-                xt = ps.tile([P, J, P], F32, name="xt", tag="xt", bufs=2)
+                xt = bank_tile("xt", [P, J, P])
                 for i in range(4):
                     w0 = 2 * i + u
                     nc.tensor.transpose(xt[:, i, :], words[:, w0:w0 + 8 * 127 + 1:8], ident[:])
                 nc.scalar.copy(out=f_v[:, u], in_=xt[:].rearrange("q t p -> q (t p)").bitcast(BF16).rearrange("q (t p e) -> q e p t", t=4, e=2))
 
-        def matmul_0(g):
-            for j in range(J):
-                r = sb.tile([P, D_IN], F32, name="r0", tag="r0", bufs=4)
-                for n in range(2):
-                    n_cols = slice(n * H, (n + 1) * H)
-                    acc = ps.tile([P, H], F32, name="acc", tag="acc", bufs=4)
-                    for q in range(2):
-                        m_cols = slice(q * H + j * P, q * H + (j + 1) * P)
-                        nc.tensor.matmul_mx(out=acc[:], lhsT=f_codes[g][:, m_cols].bitcast(E5M2X4), lhsT_scale=f_scale[g][:, m_cols],
-                                            rhs=w_codes[q][:, n_cols].bitcast(E4M3X4), rhs_scale=w_scale[q][:, n_cols],
-                                            start=(q == 0), stop=(q == 1))
-                    nc.scalar.copy(out=r[:, n_cols], in_=acc[:])
-                nc.sync.dma_start(out=o0_v[g, j], in_=r[:])
+        def matmul_0(g, j):
+            if j % 2 == 0:
+                r0[g, j // 2] = sb.tile([P, 2, D_IN], F32, name="r0_%d%d" % (g, j // 2))
+            r = r0[g, j // 2]
+            for n in range(2):
+                n_cols = slice(n * H, (n + 1) * H)
+                acc = bank_tile("acc0", [P, H])
+                for q in range(2):
+                    m_cols = slice(q * H + j * P, q * H + (j + 1) * P)
+                    nc.tensor.matmul_mx(out=acc[:], lhsT=f_codes[g][:, m_cols].bitcast(E5M2X4), lhsT_scale=f_scale[g][:, m_cols],
+                                        rhs=w_codes[q][:, n_cols].bitcast(E4M3X4), rhs_scale=w_scale[q][:, n_cols],
+                                        start=(q == 0), stop=(q == 1))
+                nc.scalar.copy(out=r[:, j % 2, n_cols], in_=acc[:])
+            if j % 2 == 1:
+                nc.sync.dma_start(out=o0_v[g][:, j - 1:j + 1, :], in_=r[:])
 
-        def make_gp(g, h):
-            cols = slice(h * H, (h + 1) * H)
-            t = sb.tile([P, J, H], F32, name="gp%d%d" % (g, h), tag="gp", bufs=3)
-            nc.vector.tensor_tensor(out=t[:], in0=g_raw[g][:, :, cols], in1=p_raw[g][:, :, cols], op=MULT)
-            gp[g, h] = t
+        def make_gp(g, u):
+            rows_u = slice(2 * u, 2 * u + 2)
+            nc.vector.tensor_tensor(out=p_raw[g][:, rows_u, :], in0=g_raw[g][:, rows_u, :], in1=p_raw[g][:, rows_u, :], op=MULT)
 
-        def sum_gp(g, h):
-            for b in range(4):
-                gt = ps.tile([P, J, P], F32, name="gt", tag=("m", "xt")[b % 2], bufs=2)
-                for j in range(J):
-                    nc.tensor.transpose(gt[:, j, :], gp[g, h][:, j, b * P:(b + 1) * P], ident[:])
-                junk = sb.tile([P, H], BF16, name="junk", tag="junk", bufs=2)
-                i = g * 8 + h * 4 + b
-                nc.scalar.activation(out=junk[:], in_=gt[:].rearrange("q j p -> q (j p)"), func=COPY, accum_out=cpart[:, i:i + 1])
+        def sum_gp(g, u):
+            for h in range(2):
+                for j in range(2 * u, 2 * u + 2):
+                    for b4 in range(4):
+                        b = 4 * h + b4
+                        nc.tensor.matmul(c_bank[h][:, b4, :], lhsT=p_raw[g][:, j, b * P:(b + 1) * P], rhs=ident[:], is_transpose=True,
+                                         start=(g == 0 and j == 0 and b4 == 0), stop=(g == 1 and j == J - 1 and b4 == 3))
+
+        def correction(h):
+            for b4 in range(4):
+                b = 4 * h + b4
+                nc.scalar.activation(out=junk[:, b, :], in_=c_bank[h][:, b4, :], func=COPY, scale=kneg[:, b:b + 1], accum_out=negc[:, b:b + 1])
 
         def matmul_1(b):
             h, b4 = divmod(b, 4)
             m_cols = slice(b * P, (b + 1) * P)
             for n in range(2):
                 n_cols = slice(n * H, (n + 1) * H)
-                acc = ps.tile([P, H], F32, name="acc", tag="acc", bufs=4)
+                acc = bank_tile("acc1", [P, H])
                 for g in range(2):
                     nc.tensor.matmul_mx(out=acc[:], lhsT=t_codes[g][:, m_cols].bitcast(E5M2X4), lhsT_scale=t_scale[g][:, m_cols],
                                         rhs=x_codes[g][:, n_cols].bitcast(E4M3X4), rhs_scale=x_scale[g][:, n_cols],
                                         start=(g == 0), stop=(g == 1))
-                w = we_raw[b][:, n_cols]
+                w = we_raw[h][:, b4, n_cols]
                 nc.vector.scalar_tensor_tensor(out=w, in0=w, scalar=negc[:, b:b + 1], in1=acc[:], op0=MULT, op1=ADD)
-                if b == 7:
-                    nc.sync.dma_start(out=o1_v[b][:, n_cols], in_=w)
-            if b < 7:
-                nc.sync.dma_start(out=o1_v[b], in_=we_raw[b])
-
-        def correction(h):
-            cols = slice(4 * h, 4 * h + 4)
-            nc.gpsimd.tensor_tensor(out=csum[:, cols], in0=cpart[:, cols], in1=cpart[:, 8 + 4 * h:12 + 4 * h], op=ADD)
-            nc.gpsimd.tensor_tensor(out=negc[:, cols], in0=csum[:, cols], in1=kneg[:, cols], op=MULT)
+            if b4 % 2 == 1:
+                nc.sync.dma_start(out=o1_v[h][:, b4 - 1:b4 + 1, :], in_=we_raw[h][:, b4 - 1:b4 + 1, :])
 
         with tc.manual_schedule():
             nc.sync.dma_start(out=norm8[:], in_=weight_norm.rearrange("(b q) -> b q", q=P))
             nc.scalar.dma_start(out=mag8[:], in_=magnitude.rearrange("a (b q) -> (a b) q", q=P))
             nc.vector.memset(rows[:], 0.0)
-            load(g_raw, 0, g_v[0], BF16, "g_raw", 2)
-            load(w_raw, 0, w_v[0], BF16, "raw", 3)
-            load(g_raw, 1, g_v[1], BF16, "g_raw", 2)
-            load(w_raw, 1, w_v[1], BF16, "raw", 3)
-            load(p_raw, 0, p_v[0], F32, "big", 3)
-            load(p_raw, 1, p_v[1], F32, "big", 3)
-            load(x_raw, 2, x_v[0], BF16, "raw", 3)
-            load(x_raw, 3, x_v[1], BF16, "raw", 3)
-            x_raw[0], x_raw[1] = x_raw[2], x_raw[3]
+            for g in range(2):
+                load(g_raw, g, g_v[g], BF16, "g_raw")
+                load(w_raw, g, w_v[g], BF16, "w_raw")
+            for g in range(2):
+                load(x_raw, g, x_v[g], BF16, "x_raw")
+            for g in range(2):
+                load(p_raw, g, p_v[g], F32, "p_raw")
             for h in range(2):
-                t = sb.tile([P, 4, D_IN], F32, name="we%d" % h, tag="big", bufs=3)
-                for b4 in range(4):
-                    b = 4 * h + b4
-                    nc.sync.dma_start(out=t[:, b4, :], in_=we_v[b])
-                    we_raw[b] = t[:, b4, :]
+                load(we_raw, h, we_v[h], F32, "we_raw")
 
             nc.vector.tensor_copy(out=rows[0:8, 0, :], in_=norm8[:])
             nc.vector.tensor_copy(out=rows[0:8, 1, :], in_=mag8[:])
-            nt = ps.tile([P, 2, P], F32, name="nt", tag="xt", bufs=2)
+            nt = ps.tile([P, 2, P], F32, name="nt", tag="bank7", bufs=1)
             nc.tensor.transpose(nt[:, 0, :], rows[:, 0, :], ident[:])
             nc.tensor.transpose(nt[:, 1, :], rows[:, 1, :], ident[:])
             nc.vector.reciprocal(out=rcol[:], in_=nt[:, 0, 0:8])
             nc.vector.tensor_tensor(out=mcol[:], in0=nt[:, 1, 0:8], in1=rcol[:], op=MULT)
             for h in range(2):
-                bank = ps.tile([P, H], F32, name="mb%d" % h, tag="m", bufs=2)
+                bank = ps.tile([P, H], F32, name="mb%d" % h, tag="bank%d" % h, bufs=1)
                 for b in range(4):
                     i = h * 4 + b
                     nc.tensor.transpose(bank[:, b * P:(b + 1) * P], mcol[:, i:i + 1].to_broadcast([P, P]), ident[:])
                 m_bank[h] = bank
+            nc.gpsimd.tensor_tensor(out=r2col[:], in0=rcol[:], in1=rcol[:], op=MULT)
+            nc.gpsimd.tensor_tensor(out=kcol[:], in0=r2col[:], in1=mcol[:], op=MULT)
+            nc.gpsimd.tensor_scalar(out=kneg[:], in0=kcol[:], scalar1=-1.0, scalar2=1.0, op0=MULT, op1=MULT)
 
             for g in range(2):
                 il_tile(w_il, g, "w_il", "il")
-            interleave("s", w_il, w_raw, 0, 0)
-            interleave("g", w_il, w_raw, 0, 1)
+            interleave("g", w_il, w_raw, 0, 0)
+            interleave("s", w_il, w_raw, 0, 1)
             interleave("g", w_il, w_raw, 1, 0)
-            interleave("g", w_il, w_raw, 1, 1)
             for g in range(2):
                 il_tile(t_il, g, "t_il", "t_il")
                 il_tile(f_il, g, "f_il", "f_il")
                 for h in range(2):
                     make_dz(g, h)
                     transpose_dz(g, h)
-            nc.gpsimd.tensor_tensor(out=r2col[:], in0=rcol[:], in1=rcol[:], op=MULT)
-            nc.gpsimd.tensor_tensor(out=kcol[:], in0=r2col[:], in1=mcol[:], op=MULT)
-            nc.gpsimd.tensor_scalar(out=kneg[:], in0=kcol[:], scalar1=-1.0, scalar2=1.0, op0=MULT, op1=MULT)
-            for g, h in ((0, 0), (0, 1), (1, 0)):
-                make_gp(g, h)
-                sum_gp(g, h)
+            interleave("v", w_il, w_raw, 1, 1)
+            for h in range(2):
+                c_bank[h] = ps.tile([P, 4, P], F32, name="cb%d" % h, tag="bank%d" % h, bufs=1)
             quantize(w_codes[0], w_scale[0], w_il[0], E4M3X4)
             quantize(f_codes[0], f_scale[0], f_il[0], E5M2X4)
             quantize(w_codes[1], w_scale[1], w_il[1], E4M3X4)
-            make_gp(1, 1)
-            matmul_0(0)
-            sum_gp(1, 1)
             for g in range(2):
                 il_tile(x_il, g, "x_il", "il")
-            interleave("v", x_il, x_raw, 0, 0)
-            quantize(f_codes[1], f_scale[1], f_il[1], E5M2X4)
-            interleave("v", x_il, x_raw, 0, 1)
+            interleave("s", x_il, x_raw, 0, 0)
+            for j in range(J):
+                matmul_0(0, j)
             quantize(t_codes[0], t_scale[0], t_il[0], E5M2X4)
-            interleave("v", x_il, x_raw, 1, 0)
-            quantize(x_codes[0], x_scale[0], x_il[0], E4M3X4)
-            interleave("v", x_il, x_raw, 1, 1)
+            quantize(f_codes[1], f_scale[1], f_il[1], E5M2X4)
+            for j in range(J):
+                matmul_0(1, j)
             quantize(t_codes[1], t_scale[1], t_il[1], E5M2X4)
-            correction(0)
+            for g in range(2):
+                for u in range(2):
+                    make_gp(g, u)
+                    sum_gp(g, u)
+            interleave("s", x_il, x_raw, 0, 1)
+            interleave("v", x_il, x_raw, 1, 0)
+            interleave("v", x_il, x_raw, 1, 1)
+            quantize(x_codes[0], x_scale[0], x_il[0], E4M3X4)
             quantize(x_codes[1], x_scale[1], x_il[1], E4M3X4)
+            correction(0)
             correction(1)
-            matmul_0(1)
             for b in range(8):
                 matmul_1(b)

@@ -29,9 +29,9 @@ def tile_loralinear_pa_v_kernel(tc, x, weight, a_w, b_w, magnitude, h_lora, pre,
     g_v = grad_out.flatten_outer_dims().rearrange("(g p j) d -> g p j d", p=P, j=J)
     p_v = pre.flatten_outer_dims().rearrange("(g p j) d -> g p j d", p=P, j=J)
     w_v = weight.rearrange("(g p j) d -> g p j d", p=P, j=J)
-    we_v = w_eff.rearrange("(h b q) d -> h q b d", q=P, b=4)
+    we_v = w_eff.rearrange("(h q t) d -> h q t d", q=P, t=J)
     o0_v = out_0.flatten_outer_dims().rearrange("(g p j) d -> g p j d", p=P, j=J)
-    o1_v = out_1.rearrange("(h b q) d -> h q b d", q=P, b=4)
+    o1_v = out_1.rearrange("(h q t) d -> h q t d", q=P, t=J)
 
     with ExitStack() as ctx:
         sb = ctx.enter_context(tc.tile_pool(name="sb", bufs=1))
@@ -46,9 +46,10 @@ def tile_loralinear_pa_v_kernel(tc, x, weight, a_w, b_w, magnitude, h_lora, pre,
         mcol = sb.tile([P, 8], F32, name="mcol")
         r2col = sb.tile([P, 8], F32, name="r2col")
         kcol = sb.tile([P, 8], F32, name="kcol")
-        kneg = sb.tile([P, 8], F32, name="kneg")
-        negc = sb.tile([P, 8], F32, name="negc")
-        junk = sb.tile([P, 8, P], BF16, name="junk")
+        kneg = sb.tile([P, J, 2], F32, name="kneg")
+        negc = sb.tile([P, J, 2], F32, name="negc")
+        k_cols = sb.tile([P, 4, P], F32, name="k_cols", tag="r0_0")
+        k_rows = sb.tile([P, H], F32, name="k_rows", tag="r0_1")
 
         t_codes = [sb.tile([P, D_OUT], U32, name="t_codes%d" % g, align_bytes=64) for g in range(2)]
         t_scale = [sb.tile([P, D_OUT], U8, name="t_scale%d" % g, align_bytes=64) for g in range(2)]
@@ -60,7 +61,7 @@ def tile_loralinear_pa_v_kernel(tc, x, weight, a_w, b_w, magnitude, h_lora, pre,
         x_scale = [sb.tile([P, D_IN], U8, name="x_scale%d" % g, align_bytes=64) for g in range(2)]
 
         g_raw, w_raw, x_raw, p_raw, we_raw = {}, {}, {}, {}, {}
-        t_il, w_il, x_il, f_il, m_bank, c_bank, r0 = {}, {}, {}, {}, {}, {}, {}
+        t_il, w_il, x_il, f_il, m_bank, c_bank, r0, gp = {}, {}, {}, {}, {}, {}, {}, {}
 
         turn = {"xt": 0, "acc0": 0, "acc1": 0}
         banks = {"xt": (2, 3, 4, 5), "acc0": (6, 7, 2, 3, 4, 5), "acc1": (2, 3, 4, 5, 6, 7, 0, 1)}
@@ -94,7 +95,7 @@ def tile_loralinear_pa_v_kernel(tc, x, weight, a_w, b_w, magnitude, h_lora, pre,
 
         def make_dz(g, h):
             cols = slice(h * H, (h + 1) * H)
-            nc.vector.tensor_tensor(out=t_il[g][:, cols, :].rearrange("p (c i) j -> p c j i", i=4),
+            nc.vector.tensor_tensor(out=t_il[g][:, cols, :].rearrange("p (i c) j -> p c j i", i=4),
                                     in0=g_raw[g][:, :, cols].rearrange("p j (c i) -> p c j i", i=4),
                                     in1=m_bank[h][:].rearrange("p (c i) -> p c i", i=4).unsqueeze(2).to_broadcast([P, H // 4, J, 4]), op=MULT)
 
@@ -104,14 +105,14 @@ def tile_loralinear_pa_v_kernel(tc, x, weight, a_w, b_w, magnitude, h_lora, pre,
             for u in range(2):
                 xt = bank_tile("xt", [P, J, P])
                 for i in range(4):
-                    w0 = 2 * i + u
-                    nc.tensor.transpose(xt[:, i, :], words[:, w0:w0 + 8 * 127 + 1:8], ident[:])
+                    w0 = 2 * P * i + u
+                    nc.tensor.transpose(xt[:, i, :], words[:, w0:w0 + 2 * (P - 1) + 1:2], ident[:])
                 nc.scalar.copy(out=f_v[:, u], in_=xt[:].rearrange("q t p -> q (t p)").bitcast(BF16).rearrange("q (t p e) -> q e p t", t=4, e=2))
 
         def matmul_0(g, j):
-            if j % 2 == 0:
-                r0[g, j // 2] = sb.tile([P, 2, D_IN], F32, name="r0_%d%d" % (g, j // 2))
-            r = r0[g, j // 2]
+            if j == 0:
+                r0[g] = sb.tile([P, J, D_IN], F32, name="r0_%d" % g)
+            r = r0[g]
             for n in range(2):
                 n_cols = slice(n * H, (n + 1) * H)
                 acc = bank_tile("acc0", [P, H])
@@ -120,26 +121,42 @@ def tile_loralinear_pa_v_kernel(tc, x, weight, a_w, b_w, magnitude, h_lora, pre,
                     nc.tensor.matmul_mx(out=acc[:], lhsT=f_codes[g][:, m_cols].bitcast(E5M2X4), lhsT_scale=f_scale[g][:, m_cols],
                                         rhs=w_codes[q][:, n_cols].bitcast(E4M3X4), rhs_scale=w_scale[q][:, n_cols],
                                         start=(q == 0), stop=(q == 1))
-                nc.scalar.copy(out=r[:, j % 2, n_cols], in_=acc[:])
-            if j % 2 == 1:
-                nc.sync.dma_start(out=o0_v[g][:, j - 1:j + 1, :], in_=r[:])
+                nc.scalar.copy(out=r[:, j, n_cols], in_=acc[:])
+            if j == J - 1:
+                nc.sync.dma_start(out=o0_v[g], in_=r[:])
 
         def make_gp(g, u):
             rows_u = slice(2 * u, 2 * u + 2)
-            nc.vector.tensor_tensor(out=p_raw[g][:, rows_u, :], in0=g_raw[g][:, rows_u, :], in1=p_raw[g][:, rows_u, :], op=MULT)
+            if g == 0:
+                gp[g, u] = sb.tile([P, 2, 2, J, P], F32, name="gp", tag="w_raw%d" % u)[:]
+            elif u == 0:
+                both = sb.tile([P, J, 2, J, P], F32, name="gp", tag="p_raw0")
+                gp[g, 0], gp[g, 1] = both[:, 0:2], both[:, 2:4]
+            nc.vector.tensor_tensor(out=gp[g, u].rearrange("p j h t q -> p (j h) q t"),
+                                    in0=g_raw[g][:, rows_u, :].rearrange("p j (h q t) -> p (j h) q t", h=2, t=J),
+                                    in1=p_raw[g][:, rows_u, :].rearrange("p j (h q t) -> p (j h) q t", h=2, t=J), op=MULT)
 
         def sum_gp(g, u):
             for h in range(2):
                 for j in range(2 * u, 2 * u + 2):
                     for b4 in range(4):
-                        b = 4 * h + b4
-                        nc.tensor.matmul(c_bank[h][:, b4, :], lhsT=p_raw[g][:, j, b * P:(b + 1) * P], rhs=ident[:], is_transpose=True,
+                        nc.tensor.matmul(c_bank[h][:, b4, :], lhsT=gp[g, u][:, j % 2, h, b4, :], rhs=ident[:], is_transpose=True,
                                          start=(g == 0 and j == 0 and b4 == 0), stop=(g == 1 and j == J - 1 and b4 == 3))
 
         def correction(h):
+            junk = sb.tile([P, 4, P], BF16, name="junk", tag="g_raw%d" % h)
             for b4 in range(4):
-                b = 4 * h + b4
-                nc.scalar.activation(out=junk[:, b, :], in_=c_bank[h][:, b4, :], func=COPY, scale=kneg[:, b:b + 1], accum_out=negc[:, b:b + 1])
+                nc.scalar.activation(out=junk[:, b4, :], in_=c_bank[h][:, b4, :], func=COPY, scale=kneg[:, b4, h:h + 1], accum_out=negc[:, b4, h:h + 1])
+
+        def reorder_factor():
+            rows_ps = ps.tile([P, 4, P], F32, name="rows_ps", tag="bank6", bufs=1)
+            for b4 in range(4):
+                nc.tensor.transpose(rows_ps[:, b4, :], k_cols[:, b4, :], ident[:])
+            nc.scalar.copy(out=k_rows[:], in_=rows_ps[:].rearrange("p b q -> p (b q)"))
+            cols_ps = ps.tile([P, J, P], F32, name="cols_ps", tag="bank7", bufs=1)
+            for t in range(J):
+                nc.tensor.transpose(cols_ps[:, t, :], k_rows[:, t:t + J * (P - 1) + 1:J], ident[:])
+            nc.scalar.copy(out=kneg[:], in_=cols_ps[:, :, 0:2])
 
         def matmul_1(b):
             h, b4 = divmod(b, 4)
@@ -152,7 +169,7 @@ def tile_loralinear_pa_v_kernel(tc, x, weight, a_w, b_w, magnitude, h_lora, pre,
                                         rhs=x_codes[g][:, n_cols].bitcast(E4M3X4), rhs_scale=x_scale[g][:, n_cols],
                                         start=(g == 0), stop=(g == 1))
                 w = we_raw[h][:, b4, n_cols]
-                nc.vector.scalar_tensor_tensor(out=w, in0=w, scalar=negc[:, b:b + 1], in1=acc[:], op0=MULT, op1=ADD)
+                nc.vector.scalar_tensor_tensor(out=w, in0=w, scalar=negc[:, b4, h:h + 1], in1=acc[:], op0=MULT, op1=ADD)
             if b4 % 2 == 1:
                 nc.sync.dma_start(out=o1_v[h][:, b4 - 1:b4 + 1, :], in_=we_raw[h][:, b4 - 1:b4 + 1, :])
 
@@ -183,9 +200,11 @@ def tile_loralinear_pa_v_kernel(tc, x, weight, a_w, b_w, magnitude, h_lora, pre,
                     i = h * 4 + b
                     nc.tensor.transpose(bank[:, b * P:(b + 1) * P], mcol[:, i:i + 1].to_broadcast([P, P]), ident[:])
                 m_bank[h] = bank
+            nc.gpsimd.memset(k_cols[:], 0.0)
             nc.gpsimd.tensor_tensor(out=r2col[:], in0=rcol[:], in1=rcol[:], op=MULT)
             nc.gpsimd.tensor_tensor(out=kcol[:], in0=r2col[:], in1=mcol[:], op=MULT)
-            nc.gpsimd.tensor_scalar(out=kneg[:], in0=kcol[:], scalar1=-1.0, scalar2=1.0, op0=MULT, op1=MULT)
+            nc.gpsimd.tensor_scalar(out=k_cols[:, :, 0:2], in0=kcol[:].rearrange("p (h b) -> p b h", h=2), scalar1=-1.0, scalar2=1.0, op0=MULT, op1=MULT)
+            reorder_factor()
 
             for g in range(2):
                 il_tile(w_il, g, "w_il", "il")

@@ -170,7 +170,11 @@ def tile_loralinear_pa_v_kernel(tc, x, weight, a_w, b_w, magnitude, h_lora, pre,
                                         start=(g == 0), stop=(g == 1))
                 w = we_raw[h][:, b4, n_cols]
                 nc.vector.scalar_tensor_tensor(out=w, in0=w, scalar=negc[:, b4, h:h + 1], in1=acc[:], op0=MULT, op1=ADD)
-            if b4 % 2 == 1:
+                if b == 7:
+                    nc.sync.dma_start(out=o1_v[h][:, b4, n_cols], in_=w)
+            if b == 6:
+                nc.sync.dma_start(out=o1_v[h][:, b4, :], in_=we_raw[h][:, b4, :])
+            elif b < 6 and b4 % 2 == 1:
                 nc.sync.dma_start(out=o1_v[h][:, b4 - 1:b4 + 1, :], in_=we_raw[h][:, b4 - 1:b4 + 1, :])
 
         with tc.manual_schedule():
@@ -238,7 +242,7 @@ def tile_loralinear_pa_v_kernel(tc, x, weight, a_w, b_w, magnitude, h_lora, pre,
                     make_gp(g, u)
                     sum_gp(g, u)
             interleave("s", x_il, x_raw, 0, 1)
-            interleave("v", x_il, x_raw, 1, 0)
+            interleave("s", x_il, x_raw, 1, 0)
             interleave("v", x_il, x_raw, 1, 1)
             quantize(x_codes[0], x_scale[0], x_il[0], E4M3X4)
             quantize(x_codes[1], x_scale[1], x_il[1], E4M3X4)

@@ -21,6 +21,7 @@ P = 128
 J = 4
 K = P * J
 H = 512
+EARLY = 3
 
 
 def tile_loralinear_pa_v_kernel(tc, x, weight, a_w, b_w, magnitude, h_lora, pre, w_eff, weight_norm, grad_out, out_0, out_1):
@@ -61,10 +62,10 @@ def tile_loralinear_pa_v_kernel(tc, x, weight, a_w, b_w, magnitude, h_lora, pre,
         x_scale = [sb.tile([P, D_IN], U8, name="x_scale%d" % g, align_bytes=64) for g in range(2)]
 
         g_raw, w_raw, x_raw, p_raw, we_raw = {}, {}, {}, {}, {}
-        t_il, w_il, x_il, f_il, m_bank, c_bank, r0, gp = {}, {}, {}, {}, {}, {}, {}, {}
+        t_il, w_il, x_il, f_il, m_bank, c_bank, r0, gp, acc1 = {}, {}, {}, {}, {}, {}, {}, {}, {}
 
         turn = {"xt": 0, "acc0": 0, "acc1": 0}
-        banks = {"xt": (2, 3, 4, 5), "acc0": (6, 7, 2, 3, 4, 5), "acc1": (2, 3, 4, 5, 6, 7, 0, 1)}
+        banks = {"xt": (2, 3, 4, 5), "acc0": (6, 7, 2, 3, 4, 5), "acc1": (4, 5, 6, 7, 2, 3, 0, 1)}
 
         def bank_tile(role, shape):
             i = banks[role][turn[role] % len(banks[role])]
@@ -122,8 +123,10 @@ def tile_loralinear_pa_v_kernel(tc, x, weight, a_w, b_w, magnitude, h_lora, pre,
                                         rhs=w_codes[q][:, n_cols].bitcast(E4M3X4), rhs_scale=w_scale[q][:, n_cols],
                                         start=(q == 0), stop=(q == 1))
                 nc.scalar.copy(out=r[:, j, n_cols], in_=acc[:])
-            if j == J - 1:
+            if g == 0 and j == J - 1:
                 nc.sync.dma_start(out=o0_v[g], in_=r[:])
+            if g == 1 and j % 2 == 1:
+                nc.sync.dma_start(out=o0_v[g][:, j - 1:j + 1, :], in_=r[:, j - 1:j + 1, :])
 
         def make_gp(g, u):
             rows_u = slice(2 * u, 2 * u + 2)
@@ -136,12 +139,11 @@ def tile_loralinear_pa_v_kernel(tc, x, weight, a_w, b_w, magnitude, h_lora, pre,
                                     in0=g_raw[g][:, rows_u, :].rearrange("p j (h q t) -> p (j h) q t", h=2, t=J),
                                     in1=p_raw[g][:, rows_u, :].rearrange("p j (h q t) -> p (j h) q t", h=2, t=J), op=MULT)
 
-        def sum_gp(g, u):
+        def sum_gp(g, j):
             for h in range(2):
-                for j in range(2 * u, 2 * u + 2):
-                    for b4 in range(4):
-                        nc.tensor.matmul(c_bank[h][:, b4, :], lhsT=gp[g, u][:, j % 2, h, b4, :], rhs=ident[:], is_transpose=True,
-                                         start=(g == 0 and j == 0 and b4 == 0), stop=(g == 1 and j == J - 1 and b4 == 3))
+                for b4 in range(4):
+                    nc.tensor.matmul(c_bank[h][:, b4, :], lhsT=gp[g, j // 2][:, j % 2, h, b4, :], rhs=ident[:], is_transpose=True,
+                                     start=(g == 0 and j == 0 and b4 == 0), stop=(g == 1 and j == J - 1 and b4 == 3))
 
         def correction(h):
             junk = sb.tile([P, 4, P], BF16, name="junk", tag="g_raw%d" % h)
@@ -153,29 +155,36 @@ def tile_loralinear_pa_v_kernel(tc, x, weight, a_w, b_w, magnitude, h_lora, pre,
             for b4 in range(4):
                 nc.tensor.transpose(rows_ps[:, b4, :], k_cols[:, b4, :], ident[:])
             nc.scalar.copy(out=k_rows[:], in_=rows_ps[:].rearrange("p b q -> p (b q)"))
+
+        def reorder_factor_back():
             cols_ps = ps.tile([P, J, P], F32, name="cols_ps", tag="bank7", bufs=1)
             for t in range(J):
                 nc.tensor.transpose(cols_ps[:, t, :], k_rows[:, t:t + J * (P - 1) + 1:J], ident[:])
             nc.scalar.copy(out=kneg[:], in_=cols_ps[:, :, 0:2])
 
+        def pass_1(b, n, g):
+            m_cols = slice(b * P, (b + 1) * P)
+            n_cols = slice(n * H, (n + 1) * H)
+            if g == 0:
+                acc1[b, n] = bank_tile("acc1", [P, H])
+            nc.tensor.matmul_mx(out=acc1[b, n][:], lhsT=t_codes[g][:, m_cols].bitcast(E5M2X4), lhsT_scale=t_scale[g][:, m_cols],
+                                rhs=x_codes[g][:, n_cols].bitcast(E4M3X4), rhs_scale=x_scale[g][:, n_cols],
+                                start=(g == 0), stop=(g == 1))
+
         def matmul_1(b):
             h, b4 = divmod(b, 4)
-            m_cols = slice(b * P, (b + 1) * P)
             for n in range(2):
                 n_cols = slice(n * H, (n + 1) * H)
-                acc = bank_tile("acc1", [P, H])
-                for g in range(2):
-                    nc.tensor.matmul_mx(out=acc[:], lhsT=t_codes[g][:, m_cols].bitcast(E5M2X4), lhsT_scale=t_scale[g][:, m_cols],
-                                        rhs=x_codes[g][:, n_cols].bitcast(E4M3X4), rhs_scale=x_scale[g][:, n_cols],
-                                        start=(g == 0), stop=(g == 1))
+                if b >= EARLY:
+                    pass_1(b, n, 0)
+                pass_1(b, n, 1)
+                acc = acc1[b, n]
                 w = we_raw[h][:, b4, n_cols]
                 nc.vector.scalar_tensor_tensor(out=w, in0=w, scalar=negc[:, b4, h:h + 1], in1=acc[:], op0=MULT, op1=ADD)
                 if b == 7:
                     nc.sync.dma_start(out=o1_v[h][:, b4, n_cols], in_=w)
-            if b == 6:
+            if b < 7:
                 nc.sync.dma_start(out=o1_v[h][:, b4, :], in_=we_raw[h][:, b4, :])
-            elif b < 6 and b4 % 2 == 1:
-                nc.sync.dma_start(out=o1_v[h][:, b4 - 1:b4 + 1, :], in_=we_raw[h][:, b4 - 1:b4 + 1, :])
 
         with tc.manual_schedule():
             nc.sync.dma_start(out=norm8[:], in_=weight_norm.rearrange("(b q) -> b q", q=P))
@@ -214,6 +223,7 @@ def tile_loralinear_pa_v_kernel(tc, x, weight, a_w, b_w, magnitude, h_lora, pre,
                 il_tile(w_il, g, "w_il", "il")
             interleave("g", w_il, w_raw, 0, 0)
             interleave("s", w_il, w_raw, 0, 1)
+            reorder_factor_back()
             interleave("g", w_il, w_raw, 1, 0)
             for g in range(2):
                 il_tile(t_il, g, "t_il", "t_il")
@@ -230,21 +240,35 @@ def tile_loralinear_pa_v_kernel(tc, x, weight, a_w, b_w, magnitude, h_lora, pre,
             for g in range(2):
                 il_tile(x_il, g, "x_il", "il")
             interleave("s", x_il, x_raw, 0, 0)
-            for j in range(J):
+            for j in range(3):
                 matmul_0(0, j)
-            quantize(t_codes[0], t_scale[0], t_il[0], E5M2X4)
+            make_gp(0, 0)
+            make_gp(0, 1)
+            sum_gp(0, 0)
+            matmul_0(0, 3)
+            sum_gp(0, 1)
             quantize(f_codes[1], f_scale[1], f_il[1], E5M2X4)
-            for j in range(J):
-                matmul_0(1, j)
-            quantize(t_codes[1], t_scale[1], t_il[1], E5M2X4)
-            for g in range(2):
-                for u in range(2):
-                    make_gp(g, u)
-                    sum_gp(g, u)
             interleave("s", x_il, x_raw, 0, 1)
+            sum_gp(0, 2)
+            matmul_0(1, 0)
+            sum_gp(0, 3)
+            make_gp(1, 0)
+            make_gp(1, 1)
+            matmul_0(1, 1)
             interleave("s", x_il, x_raw, 1, 0)
+            sum_gp(1, 0)
+            matmul_0(1, 2)
+            sum_gp(1, 1)
+            matmul_0(1, 3)
+            sum_gp(1, 2)
+            sum_gp(1, 3)
+            quantize(t_codes[0], t_scale[0], t_il[0], E5M2X4)
             interleave("v", x_il, x_raw, 1, 1)
             quantize(x_codes[0], x_scale[0], x_il[0], E4M3X4)
+            for b in range(EARLY):
+                for n in range(2):
+                    pass_1(b, n, 0)
+            quantize(t_codes[1], t_scale[1], t_il[1], E5M2X4)
             quantize(x_codes[1], x_scale[1], x_il[1], E4M3X4)
             correction(0)
             correction(1)

@@ -40,17 +40,14 @@ def tile_loralinear_pa_v_kernel(tc, x, weight, a_w, b_w, magnitude, h_lora, pre,
 
         ident = sb.tile([P, P], F32, name="ident")
         make_identity(nc, ident[:])
-        norm8 = sb.tile([8, P], F32, name="norm8")
-        mag8 = sb.tile([8, P], BF16, name="mag8")
-        rows = sb.tile([P, 2, P], F32, name="rows")
-        rcol = sb.tile([P, 8], F32, name="rcol")
-        mcol = sb.tile([P, 8], F32, name="mcol")
-        r2col = sb.tile([P, 8], F32, name="r2col")
-        kcol = sb.tile([P, 8], F32, name="kcol")
-        kneg = sb.tile([P, J, 2], F32, name="kneg")
-        negc = sb.tile([P, J, 2], F32, name="negc")
-        k_cols = sb.tile([P, 4, P], F32, name="k_cols", tag="r0_0")
-        k_rows = sb.tile([P, H], F32, name="k_rows", tag="r0_1")
+        norm = sb.tile([P, 2, 8], F32, name="norm")
+        mag = sb.tile([P, 2, 16], BF16, name="mag")
+        rcol = sb.tile([P, 2, J], F32, name="rcol")
+        mcol = sb.tile([P, 2, J], F32, name="mcol")
+        r2col = sb.tile([P, 2, J], F32, name="r2col")
+        kcol = sb.tile([P, 2, J], F32, name="kcol")
+        kneg = sb.tile([P, 2, J], F32, name="kneg")
+        negc = sb.tile([P, 2, J], F32, name="negc")
 
         t_codes = [sb.tile([P, D_OUT], U32, name="t_codes%d" % g, align_bytes=64) for g in range(2)]
         t_scale = [sb.tile([P, D_OUT], U8, name="t_scale%d" % g, align_bytes=64) for g in range(2)]
@@ -65,7 +62,7 @@ def tile_loralinear_pa_v_kernel(tc, x, weight, a_w, b_w, magnitude, h_lora, pre,
         t_il, w_il, x_il, f_il, m_bank, c_bank, r0, gp, acc1 = {}, {}, {}, {}, {}, {}, {}, {}, {}
 
         turn = {"xt": 0, "acc0": 0, "acc1": 0}
-        banks = {"xt": (2, 3, 4, 5), "acc0": (6, 7, 2, 3, 4, 5), "acc1": (4, 5, 6, 7, 2, 3, 0, 1)}
+        banks = {"xt": (2, 3, 4, 5), "acc0": (6, 7, 2, 3, 4, 5), "acc1": (4, 5, 6, 7, 0, 2, 3, 4, 5, 6, 7, 0, 1, 2, 3, 4)}
 
         def bank_tile(role, shape):
             i = banks[role][turn[role] % len(banks[role])]
@@ -98,7 +95,7 @@ def tile_loralinear_pa_v_kernel(tc, x, weight, a_w, b_w, magnitude, h_lora, pre,
             cols = slice(h * H, (h + 1) * H)
             nc.vector.tensor_tensor(out=t_il[g][:, cols, :].rearrange("p (i c) j -> p c j i", i=4),
                                     in0=g_raw[g][:, :, cols].rearrange("p j (c i) -> p c j i", i=4),
-                                    in1=m_bank[h][:].rearrange("p (c i) -> p c i", i=4).unsqueeze(2).to_broadcast([P, H // 4, J, 4]), op=MULT)
+                                    in1=m_bank[h][:].rearrange("p (i c) -> p c i", i=4).unsqueeze(2).to_broadcast([P, H // 4, J, 4]), op=MULT)
 
         def transpose_dz(g, h):
             words = t_il[g][:, h * H:(h + 1) * H, :].rearrange("p o j -> p (o j)").bitcast(F32)
@@ -128,39 +125,27 @@ def tile_loralinear_pa_v_kernel(tc, x, weight, a_w, b_w, magnitude, h_lora, pre,
             if g == 1 and j % 2 == 1:
                 nc.sync.dma_start(out=o0_v[g][:, j - 1:j + 1, :], in_=r[:, j - 1:j + 1, :])
 
-        def make_gp(g, u):
-            rows_u = slice(2 * u, 2 * u + 2)
+        def make_gp(g, h):
+            cols = slice(h * H, (h + 1) * H)
             if g == 0:
-                gp[g, u] = sb.tile([P, 2, 2, J, P], F32, name="gp", tag="w_raw%d" % u)[:]
-            elif u == 0:
-                both = sb.tile([P, J, 2, J, P], F32, name="gp", tag="p_raw0")
-                gp[g, 0], gp[g, 1] = both[:, 0:2], both[:, 2:4]
-            nc.vector.tensor_tensor(out=gp[g, u].rearrange("p j h t q -> p (j h) q t"),
-                                    in0=g_raw[g][:, rows_u, :].rearrange("p j (h q t) -> p (j h) q t", h=2, t=J),
-                                    in1=p_raw[g][:, rows_u, :].rearrange("p j (h q t) -> p (j h) q t", h=2, t=J), op=MULT)
+                gp[g, h] = sb.tile([P, J, J, P], F32, name="gp", tag="w_raw%d" % h)[:]
+            elif h == 0:
+                both = sb.tile([P, 2, J, J, P], F32, name="gp", tag="p_raw0")
+                gp[g, 0], gp[g, 1] = both[:, 0], both[:, 1]
+            nc.vector.tensor_tensor(out=gp[g, h].rearrange("p j t q -> p j q t"),
+                                    in0=g_raw[g][:, :, cols].rearrange("p j (q t) -> p j q t", t=J),
+                                    in1=p_raw[g][:, :, cols].rearrange("p j (q t) -> p j q t", t=J), op=MULT)
 
-        def sum_gp(g, j):
-            for h in range(2):
-                for b4 in range(4):
-                    nc.tensor.matmul(c_bank[h][:, b4, :], lhsT=gp[g, j // 2][:, j % 2, h, b4, :], rhs=ident[:], is_transpose=True,
-                                     start=(g == 0 and j == 0 and b4 == 0), stop=(g == 1 and j == J - 1 and b4 == 3))
+        def sum_gp(g, h, u):
+            for j in range(2 * u, 2 * u + 2):
+                for t in range(J):
+                    nc.tensor.matmul(c_bank[h][:, t, :], lhsT=gp[g, h][:, j, t, :], rhs=ident[:], is_transpose=True,
+                                     start=(g == 0 and j == 0 and t == 0), stop=(g == 1 and j == J - 1 and t == J - 1))
 
         def correction(h):
-            junk = sb.tile([P, 4, P], BF16, name="junk", tag="g_raw%d" % h)
+            junk = sb.tile([P, 4, P], BF16, name="junk", tag="x_raw%d" % h)
             for b4 in range(4):
-                nc.scalar.activation(out=junk[:, b4, :], in_=c_bank[h][:, b4, :], func=COPY, scale=kneg[:, b4, h:h + 1], accum_out=negc[:, b4, h:h + 1])
-
-        def reorder_factor():
-            rows_ps = ps.tile([P, 4, P], F32, name="rows_ps", tag="bank6", bufs=1)
-            for b4 in range(4):
-                nc.tensor.transpose(rows_ps[:, b4, :], k_cols[:, b4, :], ident[:])
-            nc.scalar.copy(out=k_rows[:], in_=rows_ps[:].rearrange("p b q -> p (b q)"))
-
-        def reorder_factor_back():
-            cols_ps = ps.tile([P, J, P], F32, name="cols_ps", tag="bank7", bufs=1)
-            for t in range(J):
-                nc.tensor.transpose(cols_ps[:, t, :], k_rows[:, t:t + J * (P - 1) + 1:J], ident[:])
-            nc.scalar.copy(out=kneg[:], in_=cols_ps[:, :, 0:2])
+                nc.scalar.activation(out=junk[:, b4, :], in_=c_bank[h][:, b4, :], func=COPY, scale=kneg[:, h, b4:b4 + 1], accum_out=negc[:, h, b4:b4 + 1])
 
         def pass_1(b, n, g):
             m_cols = slice(b * P, (b + 1) * P)
@@ -177,19 +162,18 @@ def tile_loralinear_pa_v_kernel(tc, x, weight, a_w, b_w, magnitude, h_lora, pre,
                 n_cols = slice(n * H, (n + 1) * H)
                 if b >= EARLY:
                     pass_1(b, n, 0)
-                pass_1(b, n, 1)
+                    pass_1(b, n, 1)
                 acc = acc1[b, n]
                 w = we_raw[h][:, b4, n_cols]
-                nc.vector.scalar_tensor_tensor(out=w, in0=w, scalar=negc[:, b4, h:h + 1], in1=acc[:], op0=MULT, op1=ADD)
+                nc.vector.scalar_tensor_tensor(out=w, in0=w, scalar=negc[:, h, b4:b4 + 1], in1=acc[:], op0=MULT, op1=ADD)
                 if b == 7:
                     nc.sync.dma_start(out=o1_v[h][:, b4, n_cols], in_=w)
             if b < 7:
                 nc.sync.dma_start(out=o1_v[h][:, b4, :], in_=we_raw[h][:, b4, :])
 
         with tc.manual_schedule():
-            nc.sync.dma_start(out=norm8[:], in_=weight_norm.rearrange("(b q) -> b q", q=P))
-            nc.scalar.dma_start(out=mag8[:], in_=magnitude.rearrange("a (b q) -> (a b) q", q=P))
-            nc.vector.memset(rows[:], 0.0)
+            nc.sync.dma_start(out=norm[:, :, 0:J], in_=weight_norm.rearrange("(h q t) -> q h t", h=2, t=J))
+            nc.scalar.dma_start(out=mag[:, :, 0:J], in_=magnitude.rearrange("a (h q t) -> q (a h) t", h=2, t=J))
             for g in range(2):
                 load(g_raw, g, g_v[g], BF16, "g_raw")
                 load(w_raw, g, w_v[g], BF16, "w_raw")
@@ -200,30 +184,21 @@ def tile_loralinear_pa_v_kernel(tc, x, weight, a_w, b_w, magnitude, h_lora, pre,
             for h in range(2):
                 load(we_raw, h, we_v[h], F32, "we_raw")
 
-            nc.vector.tensor_copy(out=rows[0:8, 0, :], in_=norm8[:])
-            nc.vector.tensor_copy(out=rows[0:8, 1, :], in_=mag8[:])
-            nt = ps.tile([P, 2, P], F32, name="nt", tag="bank7", bufs=1)
-            nc.tensor.transpose(nt[:, 0, :], rows[:, 0, :], ident[:])
-            nc.tensor.transpose(nt[:, 1, :], rows[:, 1, :], ident[:])
-            nc.vector.reciprocal(out=rcol[:], in_=nt[:, 0, 0:8])
-            nc.vector.tensor_tensor(out=mcol[:], in0=nt[:, 1, 0:8], in1=rcol[:], op=MULT)
+            nc.vector.reciprocal(out=rcol[:], in_=norm[:, :, 0:J])
+            nc.vector.tensor_tensor(out=mcol[:], in0=mag[:, :, 0:J], in1=rcol[:], op=MULT)
             for h in range(2):
                 bank = ps.tile([P, H], F32, name="mb%d" % h, tag="bank%d" % h, bufs=1)
-                for b in range(4):
-                    i = h * 4 + b
-                    nc.tensor.transpose(bank[:, b * P:(b + 1) * P], mcol[:, i:i + 1].to_broadcast([P, P]), ident[:])
+                for t in range(J):
+                    nc.tensor.transpose(bank[:, t * P:(t + 1) * P], mcol[:, h, t:t + 1].to_broadcast([P, P]), ident[:])
                 m_bank[h] = bank
-            nc.gpsimd.memset(k_cols[:], 0.0)
             nc.gpsimd.tensor_tensor(out=r2col[:], in0=rcol[:], in1=rcol[:], op=MULT)
             nc.gpsimd.tensor_tensor(out=kcol[:], in0=r2col[:], in1=mcol[:], op=MULT)
-            nc.gpsimd.tensor_scalar(out=k_cols[:, :, 0:2], in0=kcol[:].rearrange("p (h b) -> p b h", h=2), scalar1=-1.0, scalar2=1.0, op0=MULT, op1=MULT)
-            reorder_factor()
+            nc.gpsimd.tensor_scalar(out=kneg[:], in0=kcol[:], scalar1=-1.0, scalar2=1.0, op0=MULT, op1=MULT)
 
             for g in range(2):
                 il_tile(w_il, g, "w_il", "il")
             interleave("g", w_il, w_raw, 0, 0)
             interleave("s", w_il, w_raw, 0, 1)
-            reorder_factor_back()
             interleave("g", w_il, w_raw, 1, 0)
             for g in range(2):
                 il_tile(t_il, g, "t_il", "t_il")
@@ -242,35 +217,36 @@ def tile_loralinear_pa_v_kernel(tc, x, weight, a_w, b_w, magnitude, h_lora, pre,
             interleave("s", x_il, x_raw, 0, 0)
             for j in range(3):
                 matmul_0(0, j)
+            quantize(t_codes[0], t_scale[0], t_il[0], E5M2X4)
             make_gp(0, 0)
             make_gp(0, 1)
-            sum_gp(0, 0)
+            sum_gp(0, 0, 0)
             matmul_0(0, 3)
-            sum_gp(0, 1)
+            sum_gp(0, 0, 1)
             quantize(f_codes[1], f_scale[1], f_il[1], E5M2X4)
             interleave("s", x_il, x_raw, 0, 1)
-            sum_gp(0, 2)
-            matmul_0(1, 0)
-            sum_gp(0, 3)
-            make_gp(1, 0)
-            make_gp(1, 1)
-            matmul_0(1, 1)
             interleave("s", x_il, x_raw, 1, 0)
-            sum_gp(1, 0)
+            make_gp(1, 0)
+            sum_gp(0, 1, 0)
+            matmul_0(1, 0)
+            sum_gp(0, 1, 1)
+            matmul_0(1, 1)
+            sum_gp(1, 0, 0)
             matmul_0(1, 2)
-            sum_gp(1, 1)
+            sum_gp(1, 0, 1)
+            correction(0)
             matmul_0(1, 3)
-            sum_gp(1, 2)
-            sum_gp(1, 3)
-            quantize(t_codes[0], t_scale[0], t_il[0], E5M2X4)
             interleave("v", x_il, x_raw, 1, 1)
             quantize(x_codes[0], x_scale[0], x_il[0], E4M3X4)
-            for b in range(EARLY):
-                for n in range(2):
-                    pass_1(b, n, 0)
             quantize(t_codes[1], t_scale[1], t_il[1], E5M2X4)
             quantize(x_codes[1], x_scale[1], x_il[1], E4M3X4)
-            correction(0)
+            for b in range(EARLY):
+                for n in range(2):
+                    for g in range(2):
+                        pass_1(b, n, g)
+            make_gp(1, 1)
+            for u in range(2):
+                sum_gp(1, 1, u)
             correction(1)
             for b in range(8):
                 matmul_1(b)

@@ -40,14 +40,17 @@ def tile_loralinear_pa_v_kernel(tc, x, weight, a_w, b_w, magnitude, h_lora, pre,
 
         ident = sb.tile([P, P], F32, name="ident")
         make_identity(nc, ident[:])
-        norm = sb.tile([P, 2, 8], F32, name="norm")
-        mag = sb.tile([P, 2, 16], BF16, name="mag")
-        rcol = sb.tile([P, 2, J], F32, name="rcol")
-        mcol = sb.tile([P, 2, J], F32, name="mcol")
-        r2col = sb.tile([P, 2, J], F32, name="r2col")
-        kcol = sb.tile([P, 2, J], F32, name="kcol")
-        kneg = sb.tile([P, 2, J], F32, name="kneg")
-        negc = sb.tile([P, 2, J], F32, name="negc")
+        norm8 = sb.tile([8, P], F32, name="norm8")
+        mag8 = sb.tile([8, P], BF16, name="mag8")
+        rows = sb.tile([P, 2, P], F32, name="rows")
+        rcol = sb.tile([P, 8], F32, name="rcol")
+        mcol = sb.tile([P, 8], F32, name="mcol")
+        r2col = sb.tile([P, 8], F32, name="r2col")
+        kcol = sb.tile([P, 8], F32, name="kcol")
+        kneg = sb.tile([P, J, 2], F32, name="kneg")
+        negc = sb.tile([P, J, 2], F32, name="negc")
+        k_cols = sb.tile([P, 4, P], F32, name="k_cols", tag="r0_0")
+        k_rows = sb.tile([P, H], F32, name="k_rows", tag="r0_1")
 
         t_codes = [sb.tile([P, D_OUT], U32, name="t_codes%d" % g, align_bytes=64) for g in range(2)]
         t_scale = [sb.tile([P, D_OUT], U8, name="t_scale%d" % g, align_bytes=64) for g in range(2)]
@@ -95,7 +98,7 @@ def tile_loralinear_pa_v_kernel(tc, x, weight, a_w, b_w, magnitude, h_lora, pre,
             cols = slice(h * H, (h + 1) * H)
             nc.vector.tensor_tensor(out=t_il[g][:, cols, :].rearrange("p (i c) j -> p c j i", i=4),
                                     in0=g_raw[g][:, :, cols].rearrange("p j (c i) -> p c j i", i=4),
-                                    in1=m_bank[h][:].rearrange("p (i c) -> p c i", i=4).unsqueeze(2).to_broadcast([P, H // 4, J, 4]), op=MULT)
+                                    in1=m_bank[h][:].rearrange("p (c i) -> p c i", i=4).unsqueeze(2).to_broadcast([P, H // 4, J, 4]), op=MULT)
 
         def transpose_dz(g, h):
             words = t_il[g][:, h * H:(h + 1) * H, :].rearrange("p o j -> p (o j)").bitcast(F32)
@@ -120,10 +123,8 @@ def tile_loralinear_pa_v_kernel(tc, x, weight, a_w, b_w, magnitude, h_lora, pre,
                                         rhs=w_codes[q][:, n_cols].bitcast(E4M3X4), rhs_scale=w_scale[q][:, n_cols],
                                         start=(q == 0), stop=(q == 1))
                 nc.scalar.copy(out=r[:, j, n_cols], in_=acc[:])
-            if g == 0 and j == J - 1:
+            if j == J - 1:
                 nc.sync.dma_start(out=o0_v[g], in_=r[:])
-            if g == 1 and j % 2 == 1:
-                nc.sync.dma_start(out=o0_v[g][:, j - 1:j + 1, :], in_=r[:, j - 1:j + 1, :])
 
         def make_gp(g, h):
             cols = slice(h * H, (h + 1) * H)
@@ -143,9 +144,21 @@ def tile_loralinear_pa_v_kernel(tc, x, weight, a_w, b_w, magnitude, h_lora, pre,
                                      start=(g == 0 and j == 0 and t == 0), stop=(g == 1 and j == J - 1 and t == J - 1))
 
         def correction(h):
-            junk = sb.tile([P, 4, P], BF16, name="junk", tag="x_raw%d" % h)
+            junk = sb.tile([P, 4, P], BF16, name="junk", tag="junk", bufs=2)
             for b4 in range(4):
-                nc.scalar.activation(out=junk[:, b4, :], in_=c_bank[h][:, b4, :], func=COPY, scale=kneg[:, h, b4:b4 + 1], accum_out=negc[:, h, b4:b4 + 1])
+                nc.scalar.activation(out=junk[:, b4, :], in_=c_bank[h][:, b4, :], func=COPY, scale=kneg[:, b4, h:h + 1], accum_out=negc[:, b4, h:h + 1])
+
+        def reorder_factor():
+            rows_ps = ps.tile([P, 4, P], F32, name="rows_ps", tag="bank6", bufs=1)
+            for b4 in range(4):
+                nc.tensor.transpose(rows_ps[:, b4, :], k_cols[:, b4, :], ident[:])
+            nc.scalar.copy(out=k_rows[:], in_=rows_ps[:].rearrange("p b q -> p (b q)"))
+
+        def reorder_factor_back():
+            cols_ps = ps.tile([P, J, P], F32, name="cols_ps", tag="bank7", bufs=1)
+            for t in range(J):
+                nc.tensor.transpose(cols_ps[:, t, :], k_rows[:, t:t + J * (P - 1) + 1:J], ident[:])
+            nc.scalar.copy(out=kneg[:], in_=cols_ps[:, :, 0:2])
 
         def pass_1(b, n, g):
             m_cols = slice(b * P, (b + 1) * P)
@@ -165,40 +178,51 @@ def tile_loralinear_pa_v_kernel(tc, x, weight, a_w, b_w, magnitude, h_lora, pre,
                     pass_1(b, n, 1)
                 acc = acc1[b, n]
                 w = we_raw[h][:, b4, n_cols]
-                nc.vector.scalar_tensor_tensor(out=w, in0=w, scalar=negc[:, h, b4:b4 + 1], in1=acc[:], op0=MULT, op1=ADD)
-                if b == 7:
-                    nc.sync.dma_start(out=o1_v[h][:, b4, n_cols], in_=w)
-            if b < 7:
-                nc.sync.dma_start(out=o1_v[h][:, b4, :], in_=we_raw[h][:, b4, :])
+                nc.vector.scalar_tensor_tensor(out=w, in0=w, scalar=negc[:, b4, h:h + 1], in1=acc[:], op0=MULT, op1=ADD)
+            if b4 % 2 == 1:
+                nc.sync.dma_start(out=o1_v[h][:, b4 - 1:b4 + 1, :], in_=we_raw[h][:, b4 - 1:b4 + 1, :])
 
         with tc.manual_schedule():
-            nc.sync.dma_start(out=norm[:, :, 0:J], in_=weight_norm.rearrange("(h q t) -> q h t", h=2, t=J))
-            nc.scalar.dma_start(out=mag[:, :, 0:J], in_=magnitude.rearrange("a (h q t) -> q (a h) t", h=2, t=J))
+            nc.sync.dma_start(out=norm8[:], in_=weight_norm.rearrange("(b q) -> b q", q=P))
+            nc.scalar.dma_start(out=mag8[:], in_=magnitude.rearrange("a (b q) -> (a b) q", q=P))
+            nc.vector.memset(rows[:], 0.0)
             for g in range(2):
                 load(g_raw, g, g_v[g], BF16, "g_raw")
                 load(w_raw, g, w_v[g], BF16, "w_raw")
-            for g in range(2):
-                load(x_raw, g, x_v[g], BF16, "x_raw")
+            x_all = sb.tile([P, 2, J, D_IN], BF16, name="x_all")
+            nc.sync.dma_start(out=x_all[:], in_=x_v.rearrange("g p j d -> p g j d"))
             for g in range(2):
                 load(p_raw, g, p_v[g], F32, "p_raw")
-            for h in range(2):
-                load(we_raw, h, we_v[h], F32, "we_raw")
+            we_all = sb.tile([P, 2, J, D_IN], F32, name="we_all")
+            nc.sync.dma_start(out=we_all[:], in_=we_v.rearrange("h q t d -> q h t d"))
+            for g in range(2):
+                x_raw[g] = x_all[:, g]
+                we_raw[g] = we_all[:, g]
 
-            nc.vector.reciprocal(out=rcol[:], in_=norm[:, :, 0:J])
-            nc.vector.tensor_tensor(out=mcol[:], in0=mag[:, :, 0:J], in1=rcol[:], op=MULT)
+            nc.vector.tensor_copy(out=rows[0:8, 0, :], in_=norm8[:])
+            nc.vector.tensor_copy(out=rows[0:8, 1, :], in_=mag8[:])
+            nt = ps.tile([P, 2, P], F32, name="nt", tag="bank7", bufs=1)
+            nc.tensor.transpose(nt[:, 0, :], rows[:, 0, :], ident[:])
+            nc.tensor.transpose(nt[:, 1, :], rows[:, 1, :], ident[:])
+            nc.vector.reciprocal(out=rcol[:], in_=nt[:, 0, 0:8])
+            nc.vector.tensor_tensor(out=mcol[:], in0=nt[:, 1, 0:8], in1=rcol[:], op=MULT)
             for h in range(2):
                 bank = ps.tile([P, H], F32, name="mb%d" % h, tag="bank%d" % h, bufs=1)
-                for t in range(J):
-                    nc.tensor.transpose(bank[:, t * P:(t + 1) * P], mcol[:, h, t:t + 1].to_broadcast([P, P]), ident[:])
+                for b in range(4):
+                    i = h * 4 + b
+                    nc.tensor.transpose(bank[:, b * P:(b + 1) * P], mcol[:, i:i + 1].to_broadcast([P, P]), ident[:])
                 m_bank[h] = bank
+            nc.gpsimd.memset(k_cols[:], 0.0)
             nc.gpsimd.tensor_tensor(out=r2col[:], in0=rcol[:], in1=rcol[:], op=MULT)
             nc.gpsimd.tensor_tensor(out=kcol[:], in0=r2col[:], in1=mcol[:], op=MULT)
-            nc.gpsimd.tensor_scalar(out=kneg[:], in0=kcol[:], scalar1=-1.0, scalar2=1.0, op0=MULT, op1=MULT)
+            nc.gpsimd.tensor_scalar(out=k_cols[:, :, 0:2], in0=kcol[:].rearrange("p (h b) -> p b h", h=2), scalar1=-1.0, scalar2=1.0, op0=MULT, op1=MULT)
+            reorder_factor()
 
             for g in range(2):
                 il_tile(w_il, g, "w_il", "il")
             interleave("g", w_il, w_raw, 0, 0)
             interleave("s", w_il, w_raw, 0, 1)
+            reorder_factor_back()
             interleave("g", w_il, w_raw, 1, 0)
             for g in range(2):
                 il_tile(t_il, g, "t_il", "t_il")
@@ -234,8 +258,8 @@ def tile_loralinear_pa_v_kernel(tc, x, weight, a_w, b_w, magnitude, h_lora, pre,
             sum_gp(1, 0, 0)
             matmul_0(1, 2)
             sum_gp(1, 0, 1)
-            correction(0)
             matmul_0(1, 3)
+            correction(0)
             interleave("v", x_il, x_raw, 1, 1)
             quantize(x_codes[0], x_scale[0], x_il[0], E4M3X4)
             quantize(t_codes[1], t_scale[1], t_il[1], E5M2X4)
@@ -245,8 +269,10 @@ def tile_loralinear_pa_v_kernel(tc, x, weight, a_w, b_w, magnitude, h_lora, pre,
                     for g in range(2):
                         pass_1(b, n, g)
             make_gp(1, 1)
-            for u in range(2):
-                sum_gp(1, 1, u)
+            sum_gp(1, 1, 0)
+            for b in range(4):
+                matmul_1(b)
+            sum_gp(1, 1, 1)
             correction(1)
-            for b in range(8):
+            for b in range(4, 8):
                 matmul_1(b)

@@ -114,15 +114,18 @@ def tile_loralinear_pa_v_kernel(tc, x, weight, a_w, b_w, magnitude, h_lora, pre,
             if j == 0:
                 r0[g] = sb.tile([P, J, D_IN], F32, name="r0_%d" % g)
             r = r0[g]
+            acc = {}
             for n in range(2):
-                n_cols = slice(n * H, (n + 1) * H)
-                acc = bank_tile("acc0", [P, H])
-                for q in range(2):
-                    m_cols = slice(q * H + j * P, q * H + (j + 1) * P)
-                    nc.tensor.matmul_mx(out=acc[:], lhsT=f_codes[g][:, m_cols].bitcast(E5M2X4), lhsT_scale=f_scale[g][:, m_cols],
+                acc[n] = bank_tile("acc0", [P, H])
+            for q in range(2):
+                m_cols = slice(q * H + j * P, q * H + (j + 1) * P)
+                for n in range(2):
+                    n_cols = slice(n * H, (n + 1) * H)
+                    nc.tensor.matmul_mx(out=acc[n][:], lhsT=f_codes[g][:, m_cols].bitcast(E5M2X4), lhsT_scale=f_scale[g][:, m_cols],
                                         rhs=w_codes[q][:, n_cols].bitcast(E4M3X4), rhs_scale=w_scale[q][:, n_cols],
                                         start=(q == 0), stop=(q == 1))
-                nc.scalar.copy(out=r[:, j, n_cols], in_=acc[:])
+            for n in range(2):
+                nc.scalar.copy(out=r[:, j, n * H:(n + 1) * H], in_=acc[n][:])
             if j == J - 1:
                 nc.sync.dma_start(out=o0_v[g], in_=r[:])
 
@@ -171,11 +174,12 @@ def tile_loralinear_pa_v_kernel(tc, x, weight, a_w, b_w, magnitude, h_lora, pre,
 
         def matmul_1(b):
             h, b4 = divmod(b, 4)
+            if b >= EARLY:
+                for g in range(2):
+                    for n in range(2):
+                        pass_1(b, n, g)
             for n in range(2):
                 n_cols = slice(n * H, (n + 1) * H)
-                if b >= EARLY:
-                    pass_1(b, n, 0)
-                    pass_1(b, n, 1)
                 acc = acc1[b, n]
                 w = we_raw[h][:, b4, n_cols]
                 nc.vector.scalar_tensor_tensor(out=w, in0=w, scalar=negc[:, b4, h:h + 1], in1=acc[:], op0=MULT, op1=ADD)
@@ -265,8 +269,8 @@ def tile_loralinear_pa_v_kernel(tc, x, weight, a_w, b_w, magnitude, h_lora, pre,
             quantize(t_codes[1], t_scale[1], t_il[1], E5M2X4)
             quantize(x_codes[1], x_scale[1], x_il[1], E4M3X4)
             for b in range(EARLY):
-                for n in range(2):
-                    for g in range(2):
+                for g in range(2):
+                    for n in range(2):
                         pass_1(b, n, g)
             make_gp(1, 1)
             sum_gp(1, 1, 0)

@@ -49,8 +49,8 @@ def tile_loralinear_pa_v_kernel(tc, x, weight, a_w, b_w, magnitude, h_lora, pre,
         kcol = sb.tile([P, 8], F32, name="kcol")
         kneg = sb.tile([P, J, 2], F32, name="kneg")
         negc = sb.tile([P, J, 2], F32, name="negc")
-        k_cols = sb.tile([P, 4, P], F32, name="k_cols", tag="r0_0")
-        k_rows = sb.tile([P, H], F32, name="k_rows", tag="r0_1")
+        k_cols = sb.tile([P, 4, P], F32, name="k_cols", tag="r0_0", align_bytes=256)
+        k_rows = sb.tile([P, H], F32, name="k_rows", tag="r0_1", align_bytes=256)
 
         t_codes = [sb.tile([P, D_OUT], U32, name="t_codes%d" % g, align_bytes=64) for g in range(2)]
         t_scale = [sb.tile([P, D_OUT], U8, name="t_scale%d" % g, align_bytes=64) for g in range(2)]
@@ -73,7 +73,7 @@ def tile_loralinear_pa_v_kernel(tc, x, weight, a_w, b_w, magnitude, h_lora, pre,
             return ps.tile(shape, F32, name=role, tag="bank%d" % i, bufs=1)
 
         def load(store, key, view, dtype, name):
-            t = sb.tile([P, J, 1024], dtype, name="%s%d" % (name, key))
+            t = sb.tile([P, J, 1024], dtype, name="%s%d" % (name, key), align_bytes=256)
             nc.sync.dma_start(out=t[:], in_=view)
             store[key] = t
 
@@ -112,7 +112,7 @@ def tile_loralinear_pa_v_kernel(tc, x, weight, a_w, b_w, magnitude, h_lora, pre,
 
         def matmul_0(g, j):
             if j == 0:
-                r0[g] = sb.tile([P, J, D_IN], F32, name="r0_%d" % g)
+                r0[g] = sb.tile([P, J, D_IN], F32, name="r0_%d" % g, align_bytes=256)
             r = r0[g]
             acc = {}
             for n in range(2):
@@ -132,9 +132,9 @@ def tile_loralinear_pa_v_kernel(tc, x, weight, a_w, b_w, magnitude, h_lora, pre,
         def make_gp(g, h):
             cols = slice(h * H, (h + 1) * H)
             if g == 0:
-                gp[g, h] = sb.tile([P, J, J, P], F32, name="gp", tag="w_raw%d" % h)[:]
+                gp[g, h] = sb.tile([P, J, J, P], F32, name="gp", tag="w_raw%d" % h, align_bytes=256)[:]
             elif h == 0:
-                both = sb.tile([P, 2, J, J, P], F32, name="gp", tag="p_raw0")
+                both = sb.tile([P, 2, J, J, P], F32, name="gp", tag="p_raw0", align_bytes=256)
                 gp[g, 0], gp[g, 1] = both[:, 0], both[:, 1]
             nc.vector.tensor_tensor(out=gp[g, h].rearrange("p j t q -> p j q t"),
                                     in0=g_raw[g][:, :, cols].rearrange("p j (q t) -> p j q t", t=J),
@@ -193,11 +193,11 @@ def tile_loralinear_pa_v_kernel(tc, x, weight, a_w, b_w, magnitude, h_lora, pre,
             for g in range(2):
                 load(g_raw, g, g_v[g], BF16, "g_raw")
                 load(w_raw, g, w_v[g], BF16, "w_raw")
-            x_all = sb.tile([P, 2, J, D_IN], BF16, name="x_all")
+            x_all = sb.tile([P, 2, J, D_IN], BF16, name="x_all", align_bytes=256)
             nc.sync.dma_start(out=x_all[:], in_=x_v.rearrange("g p j d -> p g j d"))
             for g in range(2):
                 load(p_raw, g, p_v[g], F32, "p_raw")
-            we_all = sb.tile([P, 2, J, D_IN], F32, name="we_all")
+            we_all = sb.tile([P, 2, J, D_IN], F32, name="we_all", align_bytes=256)
             nc.sync.dma_start(out=we_all[:], in_=we_v.rearrange("h q t d -> q h t d"))
             for g in range(2):
                 x_raw[g] = x_all[:, g]

@@ -19,18 +19,18 @@ COPY = mybir.ActivationFunctionType.Copy
 
 P = 128
 J = 4
-K = P * J
 H = 512
 EARLY = 3
+DMA_ALIGN = 256
 
 
 def tile_loralinear_pa_v_kernel(tc, x, weight, a_w, b_w, magnitude, h_lora, pre, w_eff, weight_norm, grad_out, out_0, out_1):
     nc = tc.nc
-    x_v = x.flatten_outer_dims().rearrange("(g p j) d -> g p j d", p=P, j=J)
+    x_v = x.flatten_outer_dims().rearrange("(g p j) d -> p g j d", p=P, j=J)
     g_v = grad_out.flatten_outer_dims().rearrange("(g p j) d -> g p j d", p=P, j=J)
     p_v = pre.flatten_outer_dims().rearrange("(g p j) d -> g p j d", p=P, j=J)
     w_v = weight.rearrange("(g p j) d -> g p j d", p=P, j=J)
-    we_v = w_eff.rearrange("(h q t) d -> h q t d", q=P, t=J)
+    we_v = w_eff.rearrange("(h q t) d -> q h t d", q=P, t=J)
     o0_v = out_0.flatten_outer_dims().rearrange("(g p j) d -> g p j d", p=P, j=J)
     o1_v = out_1.rearrange("(h q t) d -> h q t d", q=P, t=J)
 
@@ -39,27 +39,27 @@ def tile_loralinear_pa_v_kernel(tc, x, weight, a_w, b_w, magnitude, h_lora, pre,
         ps = ctx.enter_context(tc.psum_pool(name="ps", bufs=1))
 
         ident = sb.tile([P, P], F32, name="ident")
-        make_identity(nc, ident[:])
-        norm8 = sb.tile([8, P], F32, name="norm8")
-        mag8 = sb.tile([8, P], BF16, name="mag8")
-        rows = sb.tile([P, 2, P], F32, name="rows")
+        ident_bf = sb.tile([P, P], BF16, name="ident_bf")
+        norm_rows = sb.tile([P, P], F32, name="norm_rows")
+        mag_rows = sb.tile([P, P], BF16, name="mag_rows")
         rcol = sb.tile([P, 8], F32, name="rcol")
         mcol = sb.tile([P, 8], F32, name="mcol")
         r2col = sb.tile([P, 8], F32, name="r2col")
         kcol = sb.tile([P, 8], F32, name="kcol")
         kneg = sb.tile([P, J, 2], F32, name="kneg")
         negc = sb.tile([P, J, 2], F32, name="negc")
-        k_cols = sb.tile([P, 4, P], F32, name="k_cols", tag="r0_0", align_bytes=256)
-        k_rows = sb.tile([P, H], F32, name="k_rows", tag="r0_1", align_bytes=256)
+        k_cols = sb.tile([P, 4, P], F32, name="k_cols", tag="r0_0", align_bytes=DMA_ALIGN)
+        k_rows = sb.tile([P, H], F32, name="k_rows", tag="r0_1", align_bytes=DMA_ALIGN)
 
-        t_codes = [sb.tile([P, D_OUT], U32, name="t_codes%d" % g, align_bytes=64) for g in range(2)]
-        t_scale = [sb.tile([P, D_OUT], U8, name="t_scale%d" % g, align_bytes=64) for g in range(2)]
-        f_codes = [sb.tile([P, T], U32, name="f_codes%d" % g, align_bytes=64) for g in range(2)]
-        f_scale = [sb.tile([P, T], U8, name="f_scale%d" % g, align_bytes=64) for g in range(2)]
-        w_codes = [sb.tile([P, D_IN], U32, name="w_codes%d" % g, align_bytes=64) for g in range(2)]
-        w_scale = [sb.tile([P, D_IN], U8, name="w_scale%d" % g, align_bytes=64) for g in range(2)]
-        x_codes = [sb.tile([P, D_IN], U32, name="x_codes%d" % g, align_bytes=64) for g in range(2)]
-        x_scale = [sb.tile([P, D_IN], U8, name="x_scale%d" % g, align_bytes=64) for g in range(2)]
+        def mx_tiles(name):
+            codes = [sb.tile([P, 1024], U32, name="%s_codes%d" % (name, g), align_bytes=64) for g in range(2)]
+            scale = [sb.tile([P, 1024], U8, name="%s_scale%d" % (name, g), align_bytes=64) for g in range(2)]
+            return codes, scale
+
+        t_codes, t_scale = mx_tiles("t")
+        f_codes, f_scale = mx_tiles("f")
+        w_codes, w_scale = mx_tiles("w")
+        x_codes, x_scale = mx_tiles("x")
 
         g_raw, w_raw, x_raw, p_raw, we_raw = {}, {}, {}, {}, {}
         t_il, w_il, x_il, f_il, m_bank, c_bank, r0, gp, acc1 = {}, {}, {}, {}, {}, {}, {}, {}, {}
@@ -73,7 +73,7 @@ def tile_loralinear_pa_v_kernel(tc, x, weight, a_w, b_w, magnitude, h_lora, pre,
             return ps.tile(shape, F32, name=role, tag="bank%d" % i, bufs=1)
 
         def load(store, key, view, dtype, name):
-            t = sb.tile([P, J, 1024], dtype, name="%s%d" % (name, key), align_bytes=256)
+            t = sb.tile([P, J, 1024], dtype, name="%s%d" % (name, key), align_bytes=DMA_ALIGN)
             nc.sync.dma_start(out=t[:], in_=view)
             store[key] = t
 
@@ -91,8 +91,8 @@ def tile_loralinear_pa_v_kernel(tc, x, weight, a_w, b_w, magnitude, h_lora, pre,
             else:
                 nc.gpsimd.tensor_scalar(out=store[g][:, cols, :], in0=raw[g][:, :, cols].rearrange("p j d -> p d j"), scalar1=1.0, scalar2=1.0, op0=MULT, op1=MULT)
 
-        def quantize(codes, scales, t, fmt):
-            nc.vector.quantize_mx(out=codes[:].bitcast(fmt), scales=scales[:], in_=t[:].rearrange("p w j -> p (w j)"))
+        def quantize(codes, scales, t, fmt, cols=slice(0, 1024)):
+            nc.vector.quantize_mx(out=codes[:, cols].bitcast(fmt), scales=scales[:, cols], in_=t[:, cols, :].rearrange("p w j -> p (w j)"))
 
         def make_dz(g, h):
             cols = slice(h * H, (h + 1) * H)
@@ -112,7 +112,7 @@ def tile_loralinear_pa_v_kernel(tc, x, weight, a_w, b_w, magnitude, h_lora, pre,
 
         def matmul_0(g, j):
             if j == 0:
-                r0[g] = sb.tile([P, J, D_IN], F32, name="r0_%d" % g, align_bytes=256)
+                r0[g] = sb.tile([P, J, D_IN], F32, name="r0_%d" % g, align_bytes=DMA_ALIGN)
             r = r0[g]
             acc = {}
             for n in range(2):
@@ -132,9 +132,9 @@ def tile_loralinear_pa_v_kernel(tc, x, weight, a_w, b_w, magnitude, h_lora, pre,
         def make_gp(g, h):
             cols = slice(h * H, (h + 1) * H)
             if g == 0:
-                gp[g, h] = sb.tile([P, J, J, P], F32, name="gp", tag="w_raw%d" % h, align_bytes=256)[:]
+                gp[g, h] = sb.tile([P, J, J, P], F32, name="gp", tag="w_raw%d" % h, align_bytes=DMA_ALIGN)[:]
             elif h == 0:
-                both = sb.tile([P, 2, J, J, P], F32, name="gp", tag="p_raw0", align_bytes=256)
+                both = sb.tile([P, 2, J, J, P], F32, name="gp", tag="p_raw0", align_bytes=DMA_ALIGN)
                 gp[g, 0], gp[g, 1] = both[:, 0], both[:, 1]
             nc.vector.tensor_tensor(out=gp[g, h].rearrange("p j t q -> p j q t"),
                                     in0=g_raw[g][:, :, cols].rearrange("p j (q t) -> p j q t", t=J),
@@ -148,8 +148,8 @@ def tile_loralinear_pa_v_kernel(tc, x, weight, a_w, b_w, magnitude, h_lora, pre,
 
         def correction(h):
             junk = sb.tile([P, 4, P], BF16, name="junk", tag="junk", bufs=2)
-            for b4 in range(4):
-                nc.scalar.activation(out=junk[:, b4, :], in_=c_bank[h][:, b4, :], func=COPY, scale=kneg[:, b4, h:h + 1], accum_out=negc[:, b4, h:h + 1])
+            for t in range(J):
+                nc.scalar.activation(out=junk[:, t, :], in_=c_bank[h][:, t, :], func=COPY, scale=kneg[:, t, h:h + 1], accum_out=negc[:, t, h:h + 1])
 
         def reorder_factor():
             rows_ps = ps.tile([P, 4, P], F32, name="rows_ps", tag="bank6", bufs=1)
@@ -173,71 +173,74 @@ def tile_loralinear_pa_v_kernel(tc, x, weight, a_w, b_w, magnitude, h_lora, pre,
                                 start=(g == 0), stop=(g == 1))
 
         def matmul_1(b):
-            h, b4 = divmod(b, 4)
+            h, t = divmod(b, 4)
             if b >= EARLY:
                 for g in range(2):
                     for n in range(2):
                         pass_1(b, n, g)
             for n in range(2):
                 n_cols = slice(n * H, (n + 1) * H)
-                acc = acc1[b, n]
-                w = we_raw[h][:, b4, n_cols]
-                nc.vector.scalar_tensor_tensor(out=w, in0=w, scalar=negc[:, b4, h:h + 1], in1=acc[:], op0=MULT, op1=ADD)
-            if b4 % 2 == 1:
-                nc.sync.dma_start(out=o1_v[h][:, b4 - 1:b4 + 1, :], in_=we_raw[h][:, b4 - 1:b4 + 1, :])
+                w = we_raw[h][:, t, n_cols]
+                nc.vector.scalar_tensor_tensor(out=w, in0=w, scalar=negc[:, t, h:h + 1], in1=acc1[b, n][:], op0=MULT, op1=ADD)
+            if t % 2 == 1:
+                nc.sync.dma_start(out=o1_v[h][:, t - 1:t + 1, :], in_=we_raw[h][:, t - 1:t + 1, :])
 
         with tc.manual_schedule():
-            nc.sync.dma_start(out=norm8[:], in_=weight_norm.rearrange("(b q) -> b q", q=P))
-            nc.scalar.dma_start(out=mag8[:], in_=magnitude.rearrange("a (b q) -> (a b) q", q=P))
-            nc.vector.memset(rows[:], 0.0)
-            for g in range(2):
-                load(g_raw, g, g_v[g], BF16, "g_raw")
-                load(w_raw, g, w_v[g], BF16, "w_raw")
-            x_all = sb.tile([P, 2, J, D_IN], BF16, name="x_all", align_bytes=256)
-            nc.sync.dma_start(out=x_all[:], in_=x_v.rearrange("g p j d -> p g j d"))
+            nc.vector.memset(norm_rows[:], 0.0)
+            nc.vector.memset(mag_rows[:], 0.0)
+            make_identity(nc, ident[:])
+            make_identity(nc, ident_bf[:])
+            load(w_raw, 0, w_v[0], BF16, "w_raw")
+            nc.sync.dma_start(out=norm_rows[0:8, :], in_=weight_norm.rearrange("(b q) -> b q", q=P))
+            nc.sync.dma_start(out=mag_rows[0:8, :], in_=magnitude.rearrange("a (b q) -> (a b) q", q=P))
+            load(g_raw, 0, g_v[0], BF16, "g_raw")
+            load(w_raw, 1, w_v[1], BF16, "w_raw")
+            load(g_raw, 1, g_v[1], BF16, "g_raw")
+            x_all = sb.tile([P, 2, J, D_IN], BF16, name="x_all", align_bytes=DMA_ALIGN)
+            nc.sync.dma_start(out=x_all[:], in_=x_v)
             for g in range(2):
                 load(p_raw, g, p_v[g], F32, "p_raw")
-            we_all = sb.tile([P, 2, J, D_IN], F32, name="we_all", align_bytes=256)
-            nc.sync.dma_start(out=we_all[:], in_=we_v.rearrange("h q t d -> q h t d"))
+            we_all = sb.tile([P, 2, J, D_IN], F32, name="we_all", align_bytes=DMA_ALIGN)
+            nc.sync.dma_start(out=we_all[:], in_=we_v)
             for g in range(2):
                 x_raw[g] = x_all[:, g]
                 we_raw[g] = we_all[:, g]
 
-            nc.vector.tensor_copy(out=rows[0:8, 0, :], in_=norm8[:])
-            nc.vector.tensor_copy(out=rows[0:8, 1, :], in_=mag8[:])
-            nt = ps.tile([P, 2, P], F32, name="nt", tag="bank7", bufs=1)
-            nc.tensor.transpose(nt[:, 0, :], rows[:, 0, :], ident[:])
-            nc.tensor.transpose(nt[:, 1, :], rows[:, 1, :], ident[:])
-            nc.vector.reciprocal(out=rcol[:], in_=nt[:, 0, 0:8])
-            nc.vector.tensor_tensor(out=mcol[:], in0=nt[:, 1, 0:8], in1=rcol[:], op=MULT)
+            for g in range(2):
+                il_tile(w_il, g, "w_il", "il")
+            interleave("v", w_il, w_raw, 0, 0)
+            interleave("s", w_il, w_raw, 0, 1)
+            norm_ps = ps.tile([P, P], F32, name="norm_ps", tag="bank7", bufs=1)
+            mag_ps = ps.tile([P, P], BF16, name="mag_ps", tag="bank6", bufs=1)
+            nc.tensor.transpose(norm_ps[:], norm_rows[:], ident[:])
+            nc.tensor.transpose(mag_ps[:], mag_rows[:], ident_bf[:])
+            nc.vector.reciprocal(out=rcol[:], in_=norm_ps[:, 0:8])
+            nc.vector.tensor_tensor(out=mcol[:], in0=mag_ps[:, 0:8], in1=rcol[:], op=MULT)
             for h in range(2):
                 bank = ps.tile([P, H], F32, name="mb%d" % h, tag="bank%d" % h, bufs=1)
                 for b in range(4):
                     i = h * 4 + b
                     nc.tensor.transpose(bank[:, b * P:(b + 1) * P], mcol[:, i:i + 1].to_broadcast([P, P]), ident[:])
                 m_bank[h] = bank
+            quantize(w_codes[0], w_scale[0], w_il[0], E4M3X4, slice(0, H))
             nc.gpsimd.memset(k_cols[:], 0.0)
             nc.gpsimd.tensor_tensor(out=r2col[:], in0=rcol[:], in1=rcol[:], op=MULT)
             nc.gpsimd.tensor_tensor(out=kcol[:], in0=r2col[:], in1=mcol[:], op=MULT)
             nc.gpsimd.tensor_scalar(out=k_cols[:, :, 0:2], in0=kcol[:].rearrange("p (h b) -> p b h", h=2), scalar1=-1.0, scalar2=1.0, op0=MULT, op1=MULT)
             reorder_factor()
-
-            for g in range(2):
-                il_tile(w_il, g, "w_il", "il")
-            interleave("g", w_il, w_raw, 0, 0)
-            interleave("s", w_il, w_raw, 0, 1)
             reorder_factor_back()
+
             interleave("g", w_il, w_raw, 1, 0)
+            interleave("g", w_il, w_raw, 1, 1)
             for g in range(2):
                 il_tile(t_il, g, "t_il", "t_il")
                 il_tile(f_il, g, "f_il", "f_il")
                 for h in range(2):
                     make_dz(g, h)
                     transpose_dz(g, h)
-            interleave("v", w_il, w_raw, 1, 1)
             for h in range(2):
                 c_bank[h] = ps.tile([P, 4, P], F32, name="cb%d" % h, tag="bank%d" % h, bufs=1)
-            quantize(w_codes[0], w_scale[0], w_il[0], E4M3X4)
+            quantize(w_codes[0], w_scale[0], w_il[0], E4M3X4, slice(H, 2 * H))
             quantize(f_codes[0], f_scale[0], f_il[0], E5M2X4)
             quantize(w_codes[1], w_scale[1], w_il[1], E4M3X4)
             for g in range(2):

@@ -22,6 +22,7 @@ J = 4
 H = 512
 EARLY = 3
 DMA_ALIGN = 256
+X_SPLIT = 256
 
 
 def tile_loralinear_pa_v_kernel(tc, x, weight, a_w, b_w, magnitude, h_lora, pre, w_eff, weight_norm, grad_out, out_0, out_1):
@@ -62,15 +63,15 @@ def tile_loralinear_pa_v_kernel(tc, x, weight, a_w, b_w, magnitude, h_lora, pre,
         x_codes, x_scale = mx_tiles("x")
 
         g_raw, w_raw, x_raw, p_raw, we_raw = {}, {}, {}, {}, {}
-        t_il, w_il, x_il, f_il, m_bank, c_bank, r0, gp, acc1 = {}, {}, {}, {}, {}, {}, {}, {}, {}
+        t_il, w_il, x_il, f_il, m_bank, c_bank, r0, gp, acc0, acc1, dz_bank = {}, {}, {}, {}, {}, {}, {}, {}, {}, {}, {}
 
-        turn = {"xt": 0, "acc0": 0, "acc1": 0}
-        banks = {"xt": (2, 3, 4, 5), "acc0": (6, 7, 2, 3, 4, 5), "acc1": (4, 5, 6, 7, 0, 2, 3, 4, 5, 6, 7, 0, 1, 2, 3, 4)}
+        turn = {"xw": 0, "acc0": 0, "acc1": 0}
+        banks = {"xw": (2, 3, 4, 5), "acc0": (6, 7, 2, 3, 4, 5), "acc1": (4, 5, 6, 7, 2, 3, 0, 4, 5, 6, 7, 2, 3, 1, 0, 4)}
 
-        def bank_tile(role, shape):
+        def bank_tile(role, shape, dtype=F32):
             i = banks[role][turn[role] % len(banks[role])]
             turn[role] = turn[role] + 1
-            return ps.tile(shape, F32, name=role, tag="bank%d" % i, bufs=1)
+            return ps.tile(shape, dtype, name=role, tag="bank%d" % i, bufs=1)
 
         def load(store, key, view, dtype, name):
             t = sb.tile([P, J, 1024], dtype, name="%s%d" % (name, key), align_bytes=DMA_ALIGN)
@@ -80,8 +81,8 @@ def tile_loralinear_pa_v_kernel(tc, x, weight, a_w, b_w, magnitude, h_lora, pre,
         def il_tile(store, g, name, tag):
             store[g] = sb.tile([P, 1024, J], BF16, name="%s%d" % (name, g), tag=tag, bufs=2, align_bytes=64)
 
-        def interleave(engine, store, raw, g, h):
-            cols = slice(h * H, (h + 1) * H)
+        def interleave(engine, store, raw, g, h, cols=None):
+            cols = cols or slice(h * H, (h + 1) * H)
             out = store[g][:, cols, :].rearrange("p (c i) j -> p c j i", i=4)
             in_ = raw[g][:, :, cols].rearrange("p j (c i) -> p c j i", i=4)
             if engine == "v":
@@ -100,34 +101,41 @@ def tile_loralinear_pa_v_kernel(tc, x, weight, a_w, b_w, magnitude, h_lora, pre,
                                     in0=g_raw[g][:, :, cols].rearrange("p j (c i) -> p c j i", i=4),
                                     in1=m_bank[h][:].rearrange("p (c i) -> p c i", i=4).unsqueeze(2).to_broadcast([P, H // 4, J, 4]), op=MULT)
 
-        def transpose_dz(g, h):
+        def transpose_words(g, h):
             words = t_il[g][:, h * H:(h + 1) * H, :].rearrange("p o j -> p (o j)").bitcast(F32)
-            f_v = f_il[g][:, h * H:(h + 1) * H, :].rearrange("q (u e p) t -> q u e p t", u=2, e=2)
             for u in range(2):
-                xt = bank_tile("xt", [P, J, P])
-                for i in range(4):
-                    w0 = 2 * P * i + u
-                    nc.tensor.transpose(xt[:, i, :], words[:, w0:w0 + 2 * (P - 1) + 1:2], ident[:])
-                nc.scalar.copy(out=f_v[:, u], in_=xt[:].rearrange("q t p -> q (t p)").bitcast(BF16).rearrange("q (t p e) -> q e p t", t=4, e=2))
+                xt = bank_tile("xw", [P, J, P])
+                for t in range(J):
+                    w0 = 2 * P * t + u
+                    nc.tensor.transpose(xt[:, t, :], words[:, w0:w0 + 2 * (P - 1) + 1:2], ident[:])
+                dz_bank[g, h, u] = xt
 
-        def matmul_0(g, j):
-            if j == 0:
-                r0[g] = sb.tile([P, J, D_IN], F32, name="r0_%d" % g, align_bytes=DMA_ALIGN)
-            r = r0[g]
-            acc = {}
+        def copy_words(g, h, u):
+            f_v = f_il[g][:, h * H:(h + 1) * H, :].rearrange("q (u e p) t -> q u e p t", u=2, e=2)
+            nc.scalar.copy(out=f_v[:, u], in_=dz_bank[g, h, u][:].rearrange("q t p -> q (t p)").bitcast(BF16).rearrange("q (t p e) -> q e p t", t=4, e=2))
+
+        def passes_0(g, j):
             for n in range(2):
-                acc[n] = bank_tile("acc0", [P, H])
+                acc0[g, j, n] = bank_tile("acc0", [P, H])
             for q in range(2):
                 m_cols = slice(q * H + j * P, q * H + (j + 1) * P)
                 for n in range(2):
                     n_cols = slice(n * H, (n + 1) * H)
-                    nc.tensor.matmul_mx(out=acc[n][:], lhsT=f_codes[g][:, m_cols].bitcast(E5M2X4), lhsT_scale=f_scale[g][:, m_cols],
+                    nc.tensor.matmul_mx(out=acc0[g, j, n][:], lhsT=f_codes[g][:, m_cols].bitcast(E5M2X4), lhsT_scale=f_scale[g][:, m_cols],
                                         rhs=w_codes[q][:, n_cols].bitcast(E4M3X4), rhs_scale=w_scale[q][:, n_cols],
                                         start=(q == 0), stop=(q == 1))
+
+        def empty_0(g, j):
+            if j == 0:
+                r0[g] = sb.tile([P, J, D_IN], F32, name="r0_%d" % g, align_bytes=DMA_ALIGN)
             for n in range(2):
-                nc.scalar.copy(out=r[:, j, n * H:(n + 1) * H], in_=acc[n][:])
+                nc.scalar.copy(out=r0[g][:, j, n * H:(n + 1) * H], in_=acc0[g, j, n][:])
             if j == J - 1:
-                nc.sync.dma_start(out=o0_v[g], in_=r[:])
+                nc.sync.dma_start(out=o0_v[g], in_=r0[g][:])
+
+        def matmul_0(g, j):
+            passes_0(g, j)
+            empty_0(g, j)
 
         def make_gp(g, h):
             cols = slice(h * H, (h + 1) * H)
@@ -140,27 +148,27 @@ def tile_loralinear_pa_v_kernel(tc, x, weight, a_w, b_w, magnitude, h_lora, pre,
                                     in0=g_raw[g][:, :, cols].rearrange("p j (q t) -> p j q t", t=J),
                                     in1=p_raw[g][:, :, cols].rearrange("p j (q t) -> p j q t", t=J), op=MULT)
 
-        def sum_gp(g, h, u):
-            for j in range(2 * u, 2 * u + 2):
+        def sum_gp(g, h):
+            for j in range(J):
                 for t in range(J):
                     nc.tensor.matmul(c_bank[h][:, t, :], lhsT=gp[g, h][:, j, t, :], rhs=ident[:], is_transpose=True,
                                      start=(g == 0 and j == 0 and t == 0), stop=(g == 1 and j == J - 1 and t == J - 1))
 
         def correction(h):
-            junk = sb.tile([P, 4, P], BF16, name="junk", tag="junk", bufs=2)
+            junk = sb.tile([P, 4, P], BF16, name="junk", tag="junk", bufs=1)
             for t in range(J):
                 nc.scalar.activation(out=junk[:, t, :], in_=c_bank[h][:, t, :], func=COPY, scale=kneg[:, t, h:h + 1], accum_out=negc[:, t, h:h + 1])
 
         def reorder_factor():
-            rows_ps = ps.tile([P, 4, P], F32, name="rows_ps", tag="bank6", bufs=1)
+            rows_ps = ps.tile([P, 4, P], F32, name="rows_ps", tag="bank7", bufs=1)
             for b4 in range(4):
                 nc.tensor.transpose(rows_ps[:, b4, :], k_cols[:, b4, :], ident[:])
-            nc.scalar.copy(out=k_rows[:], in_=rows_ps[:].rearrange("p b q -> p (b q)"))
+            nc.scalar.copy(out=k_rows[:].rearrange("p (t q) -> p t q", t=J), in_=rows_ps[:].rearrange("p b c -> p (b c)").rearrange("p (q t) -> p t q", t=J))
 
         def reorder_factor_back():
-            cols_ps = ps.tile([P, J, P], F32, name="cols_ps", tag="bank7", bufs=1)
+            cols_ps = ps.tile([P, J, P], F32, name="cols_ps", tag="bank0", bufs=1)
             for t in range(J):
-                nc.tensor.transpose(cols_ps[:, t, :], k_rows[:, t:t + J * (P - 1) + 1:J], ident[:])
+                nc.tensor.transpose(cols_ps[:, t, :], k_rows[:, t * P:(t + 1) * P], ident[:])
             nc.scalar.copy(out=kneg[:], in_=cols_ps[:, :, 0:2])
 
         def pass_1(b, n, g):
@@ -172,12 +180,8 @@ def tile_loralinear_pa_v_kernel(tc, x, weight, a_w, b_w, magnitude, h_lora, pre,
                                 rhs=x_codes[g][:, n_cols].bitcast(E4M3X4), rhs_scale=x_scale[g][:, n_cols],
                                 start=(g == 0), stop=(g == 1))
 
-        def matmul_1(b):
+        def finish_1(b):
             h, t = divmod(b, 4)
-            if b >= EARLY:
-                for g in range(2):
-                    for n in range(2):
-                        pass_1(b, n, g)
             for n in range(2):
                 n_cols = slice(n * H, (n + 1) * H)
                 w = we_raw[h][:, t, n_cols]
@@ -189,7 +193,8 @@ def tile_loralinear_pa_v_kernel(tc, x, weight, a_w, b_w, magnitude, h_lora, pre,
             nc.vector.memset(norm_rows[:], 0.0)
             nc.vector.memset(mag_rows[:], 0.0)
             make_identity(nc, ident[:])
-            make_identity(nc, ident_bf[:])
+            nc.scalar.copy(out=ident_bf[:], in_=ident[:])
+            nc.gpsimd.memset(k_cols[:], 0.0)
             load(w_raw, 0, w_v[0], BF16, "w_raw")
             nc.sync.dma_start(out=norm_rows[0:8, :], in_=weight_norm.rearrange("(b q) -> b q", q=P))
             nc.sync.dma_start(out=mag_rows[0:8, :], in_=magnitude.rearrange("a (b q) -> (a b) q", q=P))
@@ -208,6 +213,8 @@ def tile_loralinear_pa_v_kernel(tc, x, weight, a_w, b_w, magnitude, h_lora, pre,
 
             for g in range(2):
                 il_tile(w_il, g, "w_il", "il")
+                il_tile(t_il, g, "t_il", "t_il")
+                il_tile(f_il, g, "f_il", "f_il")
             interleave("v", w_il, w_raw, 0, 0)
             interleave("s", w_il, w_raw, 0, 1)
             norm_ps = ps.tile([P, P], F32, name="norm_ps", tag="bank7", bufs=1)
@@ -222,64 +229,63 @@ def tile_loralinear_pa_v_kernel(tc, x, weight, a_w, b_w, magnitude, h_lora, pre,
                     i = h * 4 + b
                     nc.tensor.transpose(bank[:, b * P:(b + 1) * P], mcol[:, i:i + 1].to_broadcast([P, P]), ident[:])
                 m_bank[h] = bank
-            quantize(w_codes[0], w_scale[0], w_il[0], E4M3X4, slice(0, H))
-            nc.gpsimd.memset(k_cols[:], 0.0)
             nc.gpsimd.tensor_tensor(out=r2col[:], in0=rcol[:], in1=rcol[:], op=MULT)
             nc.gpsimd.tensor_tensor(out=kcol[:], in0=r2col[:], in1=mcol[:], op=MULT)
             nc.gpsimd.tensor_scalar(out=k_cols[:, :, 0:2], in0=kcol[:].rearrange("p (h b) -> p b h", h=2), scalar1=-1.0, scalar2=1.0, op0=MULT, op1=MULT)
-            reorder_factor()
-            reorder_factor_back()
 
+            for h in range(2):
+                quantize(w_codes[0], w_scale[0], w_il[0], E4M3X4, slice(h * H, (h + 1) * H))
             interleave("g", w_il, w_raw, 1, 0)
             interleave("g", w_il, w_raw, 1, 1)
+            reorder_factor()
             for g in range(2):
-                il_tile(t_il, g, "t_il", "t_il")
-                il_tile(f_il, g, "f_il", "f_il")
                 for h in range(2):
                     make_dz(g, h)
-                    transpose_dz(g, h)
-            for h in range(2):
-                c_bank[h] = ps.tile([P, 4, P], F32, name="cb%d" % h, tag="bank%d" % h, bufs=1)
-            quantize(w_codes[0], w_scale[0], w_il[0], E4M3X4, slice(H, 2 * H))
+                    transpose_words(g, h)
+                    copy_words(g, h, 0)
+                    copy_words(g, h, 1)
+            il_tile(x_il, 0, "x_il", "il")
             quantize(f_codes[0], f_scale[0], f_il[0], E5M2X4)
             quantize(w_codes[1], w_scale[1], w_il[1], E4M3X4)
-            for g in range(2):
-                il_tile(x_il, g, "x_il", "il")
-            interleave("s", x_il, x_raw, 0, 0)
-            for j in range(3):
-                matmul_0(0, j)
+            il_tile(x_il, 1, "x_il", "il")
             quantize(t_codes[0], t_scale[0], t_il[0], E5M2X4)
+            quantize(t_codes[1], t_scale[1], t_il[1], E5M2X4)
+            matmul_0(0, 0)
+            passes_0(0, 1)
+            passes_0(0, 2)
+            interleave("s", x_il, x_raw, 0, 0)
+            empty_0(0, 1)
+            reorder_factor_back()
+            empty_0(0, 2)
+            matmul_0(0, 3)
+            for h in range(2):
+                c_bank[h] = ps.tile([P, 4, P], F32, name="cb%d" % h, tag="bank%d" % h, bufs=1)
+            quantize(f_codes[1], f_scale[1], f_il[1], E5M2X4)
             make_gp(0, 0)
             make_gp(0, 1)
-            sum_gp(0, 0, 0)
-            matmul_0(0, 3)
-            sum_gp(0, 0, 1)
-            quantize(f_codes[1], f_scale[1], f_il[1], E5M2X4)
             interleave("s", x_il, x_raw, 0, 1)
-            interleave("s", x_il, x_raw, 1, 0)
+            interleave("s", x_il, x_raw, 1, 0, slice(0, X_SPLIT))
+            passes_0(1, 0)
+            sum_gp(0, 0)
+            passes_0(1, 1)
+            sum_gp(0, 1)
+            passes_0(1, 2)
             make_gp(1, 0)
-            sum_gp(0, 1, 0)
-            matmul_0(1, 0)
-            sum_gp(0, 1, 1)
-            matmul_0(1, 1)
-            sum_gp(1, 0, 0)
-            matmul_0(1, 2)
-            sum_gp(1, 0, 1)
-            matmul_0(1, 3)
+            empty_0(1, 0)
+            passes_0(1, 3)
+            sum_gp(1, 0)
+            for j in range(1, J):
+                empty_0(1, j)
             correction(0)
-            interleave("v", x_il, x_raw, 1, 1)
+            interleave("v", x_il, x_raw, 1, 1, slice(X_SPLIT, D_IN))
             quantize(x_codes[0], x_scale[0], x_il[0], E4M3X4)
-            quantize(t_codes[1], t_scale[1], t_il[1], E5M2X4)
             quantize(x_codes[1], x_scale[1], x_il[1], E4M3X4)
-            for b in range(EARLY):
+            make_gp(1, 1)
+            for b in range(8):
+                if b == EARLY:
+                    sum_gp(1, 1)
+                    correction(1)
                 for g in range(2):
                     for n in range(2):
                         pass_1(b, n, g)
-            make_gp(1, 1)
-            sum_gp(1, 1, 0)
-            for b in range(4):
-                matmul_1(b)
-            sum_gp(1, 1, 1)
-            correction(1)
-            for b in range(4, 8):
-                matmul_1(b)
+                finish_1(b)

from contextlib import ExitStack

import concourse.mybir as mybir
from concourse.masks import make_identity

T, D_IN, D_OUT = 1024, 1024, 1024
FLOPS = 2 * 2 * T * D_IN * D_OUT
BYTES = 2 * (T * D_IN + D_OUT * D_IN + T * D_OUT + D_OUT) + 4 * (T * D_OUT + D_OUT * D_IN + D_OUT) + 4 * (T * D_IN + D_OUT * D_IN)

F32 = mybir.dt.float32
BF16 = mybir.dt.bfloat16
U32 = mybir.dt.uint32
U8 = mybir.dt.uint8
E4M3X4 = mybir.dt.float8_e4m3fn_x4
E5M2X4 = mybir.dt.float8_e5m2_x4
MULT = mybir.AluOpType.mult
ADD = mybir.AluOpType.add
COPY = mybir.ActivationFunctionType.Copy

P = 128
J = 4
H = 512
EARLY = 3
DMA_ALIGN = 256
X_SPLIT = 256


def tile_loralinear_pa_v_kernel(tc, x, weight, a_w, b_w, magnitude, h_lora, pre, w_eff, weight_norm, grad_out, out_0, out_1):
    nc = tc.nc
    x_v = x.flatten_outer_dims().rearrange("(g p j) d -> p g j d", p=P, j=J)
    g_v = grad_out.flatten_outer_dims().rearrange("(g p j) d -> g p j d", p=P, j=J)
    p_v = pre.flatten_outer_dims().rearrange("(g p j) d -> g p j d", p=P, j=J)
    w_v = weight.rearrange("(g p j) d -> g p j d", p=P, j=J)
    we_v = w_eff.rearrange("(h q t) d -> q h t d", q=P, t=J)
    o0_v = out_0.flatten_outer_dims().rearrange("(g p j) d -> g p j d", p=P, j=J)
    o1_v = out_1.rearrange("(h q t) d -> h q t d", q=P, t=J)

    with ExitStack() as ctx:
        sb = ctx.enter_context(tc.tile_pool(name="sb", bufs=1))
        ps = ctx.enter_context(tc.psum_pool(name="ps", bufs=1))

        ident = sb.tile([P, P], F32, name="ident")
        ident_bf = sb.tile([P, P], BF16, name="ident_bf")
        norm_rows = sb.tile([P, P], F32, name="norm_rows")
        mag_rows = sb.tile([P, P], BF16, name="mag_rows")
        rcol = sb.tile([P, 8], F32, name="rcol")
        mcol = sb.tile([P, 8], F32, name="mcol")
        r2col = sb.tile([P, 8], F32, name="r2col")
        kcol = sb.tile([P, 8], F32, name="kcol")
        kneg = sb.tile([P, J, 2], F32, name="kneg")
        negc = sb.tile([P, J, 2], F32, name="negc")
        k_cols = sb.tile([P, 4, P], F32, name="k_cols", tag="r0_0", align_bytes=DMA_ALIGN)
        k_rows = sb.tile([P, H], F32, name="k_rows", tag="r0_1", align_bytes=DMA_ALIGN)

        def mx_tiles(name):
            codes = [sb.tile([P, 1024], U32, name="%s_codes%d" % (name, g), align_bytes=64) for g in range(2)]
            scale = [sb.tile([P, 1024], U8, name="%s_scale%d" % (name, g), align_bytes=64) for g in range(2)]
            return codes, scale

        t_codes, t_scale = mx_tiles("t")
        f_codes, f_scale = mx_tiles("f")
        w_codes, w_scale = mx_tiles("w")
        x_codes, x_scale = mx_tiles("x")

        g_raw, w_raw, x_raw, p_raw, we_raw = {}, {}, {}, {}, {}
        t_il, w_il, x_il, f_il, m_bank, c_bank, r0, gp, acc0, acc1, dz_bank = {}, {}, {}, {}, {}, {}, {}, {}, {}, {}, {}

        turn = {"xw": 0, "acc0": 0, "acc1": 0}
        banks = {"xw": (2, 3, 4, 5), "acc0": (6, 7, 2, 3, 4, 5), "acc1": (4, 5, 6, 7, 2, 3, 0, 4, 5, 6, 7, 2, 3, 1, 0, 4)}

        def bank_tile(role, shape, dtype=F32):
            i = banks[role][turn[role] % len(banks[role])]
            turn[role] = turn[role] + 1
            return ps.tile(shape, dtype, name=role, tag="bank%d" % i, bufs=1)

        def load(store, key, view, dtype, name):
            t = sb.tile([P, J, 1024], dtype, name="%s%d" % (name, key), align_bytes=DMA_ALIGN)
            nc.sync.dma_start(out=t[:], in_=view)
            store[key] = t

        def il_tile(store, g, name, tag):
            store[g] = sb.tile([P, 1024, J], BF16, name="%s%d" % (name, g), tag=tag, bufs=2, align_bytes=64)

        def interleave(engine, store, raw, g, h, cols=None):
            cols = cols or slice(h * H, (h + 1) * H)
            out = store[g][:, cols, :].rearrange("p (c i) j -> p c j i", i=4)
            in_ = raw[g][:, :, cols].rearrange("p j (c i) -> p c j i", i=4)
            if engine == "v":
                nc.vector.tensor_copy(out=out, in_=in_)
            elif engine == "s":
                nc.scalar.copy(out=out, in_=in_)
            else:
                nc.gpsimd.tensor_scalar(out=store[g][:, cols, :], in0=raw[g][:, :, cols].rearrange("p j d -> p d j"), scalar1=1.0, scalar2=1.0, op0=MULT, op1=MULT)

        def quantize(codes, scales, t, fmt, cols=slice(0, 1024)):
            nc.vector.quantize_mx(out=codes[:, cols].bitcast(fmt), scales=scales[:, cols], in_=t[:, cols, :].rearrange("p w j -> p (w j)"))

        def make_dz(g, h):
            cols = slice(h * H, (h + 1) * H)
            nc.vector.tensor_tensor(out=t_il[g][:, cols, :].rearrange("p (i c) j -> p c j i", i=4),
                                    in0=g_raw[g][:, :, cols].rearrange("p j (c i) -> p c j i", i=4),
                                    in1=m_bank[h][:].rearrange("p (c i) -> p c i", i=4).unsqueeze(2).to_broadcast([P, H // 4, J, 4]), op=MULT)

        def transpose_words(g, h):
            words = t_il[g][:, h * H:(h + 1) * H, :].rearrange("p o j -> p (o j)").bitcast(F32)
            for u in range(2):
                xt = bank_tile("xw", [P, J, P])
                for t in range(J):
                    w0 = 2 * P * t + u
                    nc.tensor.transpose(xt[:, t, :], words[:, w0:w0 + 2 * (P - 1) + 1:2], ident[:])
                dz_bank[g, h, u] = xt

        def copy_words(g, h, u):
            f_v = f_il[g][:, h * H:(h + 1) * H, :].rearrange("q (u e p) t -> q u e p t", u=2, e=2)
            nc.scalar.copy(out=f_v[:, u], in_=dz_bank[g, h, u][:].rearrange("q t p -> q (t p)").bitcast(BF16).rearrange("q (t p e) -> q e p t", t=4, e=2))

        def passes_0(g, j):
            for n in range(2):
                acc0[g, j, n] = bank_tile("acc0", [P, H])
            for q in range(2):
                m_cols = slice(q * H + j * P, q * H + (j + 1) * P)
                for n in range(2):
                    n_cols = slice(n * H, (n + 1) * H)
                    nc.tensor.matmul_mx(out=acc0[g, j, n][:], lhsT=f_codes[g][:, m_cols].bitcast(E5M2X4), lhsT_scale=f_scale[g][:, m_cols],
                                        rhs=w_codes[q][:, n_cols].bitcast(E4M3X4), rhs_scale=w_scale[q][:, n_cols],
                                        start=(q == 0), stop=(q == 1))

        def empty_0(g, j):
            if j == 0:
                r0[g] = sb.tile([P, J, D_IN], F32, name="r0_%d" % g, align_bytes=DMA_ALIGN)
            for n in range(2):
                nc.scalar.copy(out=r0[g][:, j, n * H:(n + 1) * H], in_=acc0[g, j, n][:])
            if j == J - 1:
                nc.sync.dma_start(out=o0_v[g], in_=r0[g][:])

        def matmul_0(g, j):
            passes_0(g, j)
            empty_0(g, j)

        def make_gp(g, h):
            cols = slice(h * H, (h + 1) * H)
            if g == 0:
                gp[g, h] = sb.tile([P, J, J, P], F32, name="gp", tag="w_raw%d" % h, align_bytes=DMA_ALIGN)[:]
            elif h == 0:
                both = sb.tile([P, 2, J, J, P], F32, name="gp", tag="p_raw0", align_bytes=DMA_ALIGN)
                gp[g, 0], gp[g, 1] = both[:, 0], both[:, 1]
            nc.vector.tensor_tensor(out=gp[g, h].rearrange("p j t q -> p j q t"),
                                    in0=g_raw[g][:, :, cols].rearrange("p j (q t) -> p j q t", t=J),
                                    in1=p_raw[g][:, :, cols].rearrange("p j (q t) -> p j q t", t=J), op=MULT)

        def sum_gp(g, h):
            for j in range(J):
                for t in range(J):
                    nc.tensor.matmul(c_bank[h][:, t, :], lhsT=gp[g, h][:, j, t, :], rhs=ident[:], is_transpose=True,
                                     start=(g == 0 and j == 0 and t == 0), stop=(g == 1 and j == J - 1 and t == J - 1))

        def correction(h):
            junk = sb.tile([P, 4, P], BF16, name="junk", tag="junk", bufs=1)
            for t in range(J):
                nc.scalar.activation(out=junk[:, t, :], in_=c_bank[h][:, t, :], func=COPY, scale=kneg[:, t, h:h + 1], accum_out=negc[:, t, h:h + 1])

        def reorder_factor():
            rows_ps = ps.tile([P, 4, P], F32, name="rows_ps", tag="bank7", bufs=1)
            for b4 in range(4):
                nc.tensor.transpose(rows_ps[:, b4, :], k_cols[:, b4, :], ident[:])
            nc.scalar.copy(out=k_rows[:].rearrange("p (t q) -> p t q", t=J), in_=rows_ps[:].rearrange("p b c -> p (b c)").rearrange("p (q t) -> p t q", t=J))

        def reorder_factor_back():
            cols_ps = ps.tile([P, J, P], F32, name="cols_ps", tag="bank0", bufs=1)
            for t in range(J):
                nc.tensor.transpose(cols_ps[:, t, :], k_rows[:, t * P:(t + 1) * P], ident[:])
            nc.scalar.copy(out=kneg[:], in_=cols_ps[:, :, 0:2])

        def pass_1(b, n, g):
            m_cols = slice(b * P, (b + 1) * P)
            n_cols = slice(n * H, (n + 1) * H)
            if g == 0:
                acc1[b, n] = bank_tile("acc1", [P, H])
            nc.tensor.matmul_mx(out=acc1[b, n][:], lhsT=t_codes[g][:, m_cols].bitcast(E5M2X4), lhsT_scale=t_scale[g][:, m_cols],
                                rhs=x_codes[g][:, n_cols].bitcast(E4M3X4), rhs_scale=x_scale[g][:, n_cols],
                                start=(g == 0), stop=(g == 1))

        def finish_1(b):
            h, t = divmod(b, 4)
            for n in range(2):
                n_cols = slice(n * H, (n + 1) * H)
                w = we_raw[h][:, t, n_cols]
                nc.vector.scalar_tensor_tensor(out=w, in0=w, scalar=negc[:, t, h:h + 1], in1=acc1[b, n][:], op0=MULT, op1=ADD)
            if t % 2 == 1:
                nc.sync.dma_start(out=o1_v[h][:, t - 1:t + 1, :], in_=we_raw[h][:, t - 1:t + 1, :])

        with tc.manual_schedule():
            nc.vector.memset(norm_rows[:], 0.0)
            nc.vector.memset(mag_rows[:], 0.0)
            make_identity(nc, ident[:])
            nc.scalar.copy(out=ident_bf[:], in_=ident[:])
            nc.gpsimd.memset(k_cols[:], 0.0)
            load(w_raw, 0, w_v[0], BF16, "w_raw")
            nc.sync.dma_start(out=norm_rows[0:8, :], in_=weight_norm.rearrange("(b q) -> b q", q=P))
            nc.sync.dma_start(out=mag_rows[0:8, :], in_=magnitude.rearrange("a (b q) -> (a b) q", q=P))
            load(g_raw, 0, g_v[0], BF16, "g_raw")
            load(w_raw, 1, w_v[1], BF16, "w_raw")
            load(g_raw, 1, g_v[1], BF16, "g_raw")
            x_all = sb.tile([P, 2, J, D_IN], BF16, name="x_all", align_bytes=DMA_ALIGN)
            nc.sync.dma_start(out=x_all[:], in_=x_v)
            for g in range(2):
                load(p_raw, g, p_v[g], F32, "p_raw")
            we_all = sb.tile([P, 2, J, D_IN], F32, name="we_all", align_bytes=DMA_ALIGN)
            nc.sync.dma_start(out=we_all[:], in_=we_v)
            for g in range(2):
                x_raw[g] = x_all[:, g]
                we_raw[g] = we_all[:, g]

            for g in range(2):
                il_tile(w_il, g, "w_il", "il")
                il_tile(t_il, g, "t_il", "t_il")
                il_tile(f_il, g, "f_il", "f_il")
            interleave("v", w_il, w_raw, 0, 0)
            interleave("s", w_il, w_raw, 0, 1)
            norm_ps = ps.tile([P, P], F32, name="norm_ps", tag="bank7", bufs=1)
            mag_ps = ps.tile([P, P], BF16, name="mag_ps", tag="bank6", bufs=1)
            nc.tensor.transpose(norm_ps[:], norm_rows[:], ident[:])
            nc.tensor.transpose(mag_ps[:], mag_rows[:], ident_bf[:])
            nc.vector.reciprocal(out=rcol[:], in_=norm_ps[:, 0:8])
            nc.vector.tensor_tensor(out=mcol[:], in0=mag_ps[:, 0:8], in1=rcol[:], op=MULT)
            for h in range(2):
                bank = ps.tile([P, H], F32, name="mb%d" % h, tag="bank%d" % h, bufs=1)
                for b in range(4):
                    i = h * 4 + b
                    nc.tensor.transpose(bank[:, b * P:(b + 1) * P], mcol[:, i:i + 1].to_broadcast([P, P]), ident[:])
                m_bank[h] = bank
            nc.gpsimd.tensor_tensor(out=r2col[:], in0=rcol[:], in1=rcol[:], op=MULT)
            nc.gpsimd.tensor_tensor(out=kcol[:], in0=r2col[:], in1=mcol[:], op=MULT)
            nc.gpsimd.tensor_scalar(out=k_cols[:, :, 0:2], in0=kcol[:].rearrange("p (h b) -> p b h", h=2), scalar1=-1.0, scalar2=1.0, op0=MULT, op1=MULT)

            for h in range(2):
                quantize(w_codes[0], w_scale[0], w_il[0], E4M3X4, slice(h * H, (h + 1) * H))
            interleave("g", w_il, w_raw, 1, 0)
            interleave("g", w_il, w_raw, 1, 1)
            reorder_factor()
            for g in range(2):
                for h in range(2):
                    make_dz(g, h)
                    transpose_words(g, h)
                    copy_words(g, h, 0)
                    copy_words(g, h, 1)
            il_tile(x_il, 0, "x_il", "il")
            quantize(f_codes[0], f_scale[0], f_il[0], E5M2X4)
            quantize(w_codes[1], w_scale[1], w_il[1], E4M3X4)
            il_tile(x_il, 1, "x_il", "il")
            quantize(t_codes[0], t_scale[0], t_il[0], E5M2X4)
            quantize(t_codes[1], t_scale[1], t_il[1], E5M2X4)
            matmul_0(0, 0)
            passes_0(0, 1)
            passes_0(0, 2)
            interleave("s", x_il, x_raw, 0, 0)
            empty_0(0, 1)
            reorder_factor_back()
            empty_0(0, 2)
            matmul_0(0, 3)
            for h in range(2):
                c_bank[h] = ps.tile([P, 4, P], F32, name="cb%d" % h, tag="bank%d" % h, bufs=1)
            quantize(f_codes[1], f_scale[1], f_il[1], E5M2X4)
            make_gp(0, 0)
            make_gp(0, 1)
            interleave("s", x_il, x_raw, 0, 1)
            interleave("s", x_il, x_raw, 1, 0, slice(0, X_SPLIT))
            passes_0(1, 0)
            sum_gp(0, 0)
            passes_0(1, 1)
            sum_gp(0, 1)
            passes_0(1, 2)
            make_gp(1, 0)
            empty_0(1, 0)
            passes_0(1, 3)
            sum_gp(1, 0)
            for j in range(1, J):
                empty_0(1, j)
            correction(0)
            interleave("v", x_il, x_raw, 1, 1, slice(X_SPLIT, D_IN))
            quantize(x_codes[0], x_scale[0], x_il[0], E4M3X4)
            quantize(x_codes[1], x_scale[1], x_il[1], E4M3X4)
            make_gp(1, 1)
            for b in range(8):
                if b == EARLY:
                    sum_gp(1, 1)
                    correction(1)
                for g in range(2):
                    for n in range(2):
                        pass_1(b, n, g)
                finish_1(b)
